import numpy as np
import ml_dtypes


def mxq(x, axis, fmt="e4m3"):
    dtype, down = {"e4m3": (ml_dtypes.float8_e4m3fn, 7), "e5m2": (ml_dtypes.float8_e5m2, 14)}[fmt]
    v = np.moveaxis(np.asarray(x, np.float32).astype(ml_dtypes.bfloat16).astype(np.float64), axis, -1)
    blocks = v.reshape(v.shape[:-1] + (-1, 32))
    amax = np.abs(blocks).max(-1, keepdims=True)
    byte = np.maximum(np.where(amax > 0, np.frexp(amax)[1] - 1 + 127, 0) - down, 1)
    scale = np.exp2(byte - 127.0)
    codes = (blocks / scale).astype(np.float32).astype(dtype).astype(np.float64)
    return np.moveaxis((codes * scale).reshape(v.shape), -1, axis)


WIDE = False


def mx_kscale(k):
    if not WIDE:
        return np.ones(k)
    levels = np.array([10, -10, 5, -5, 0])
    a = np.random.permutation(np.resize(levels, k // 512 * 4)).reshape(k // 512, 4)
    idx = np.arange(k)
    return np.exp2(a[idx // 512, idx % 128 // 32])


BF16 = ml_dtypes.bfloat16


def bf(x):
    return np.asarray(x, np.float32).astype(BF16)


def f64(x):
    return np.asarray(x).astype(np.float64)


B, S, HID, H, KV, D = 1, 4096, 1024, 2, 1, 128
EPS = 1e-6
THETA = 10000.0
HALF = D // 2


def rotate_half(x):
    return np.concatenate([-x[..., HALF:], x[..., :HALF]], axis=-1)


def rms_norm(x, w=None):
    n = x * (1.0 / np.sqrt(np.mean(x * x, axis=-1, keepdims=True) + EPS))
    return n if w is None else n * w


def setup_inputs():
    s = mx_kscale(HID)
    c = 0.004 / np.sqrt(HID)
    inv_freq = 1.0 / THETA ** (np.arange(0, D, 2) / D)
    pos = np.random.randint(0, S) + np.arange(S)
    freqs = pos[:, None] * inv_freq[None, :]
    emb = np.concatenate([freqs, freqs], axis=-1)
    return {"hidden_states": bf(np.random.standard_normal((B, S, HID)) * s),
            "cos": bf(np.cos(emb)[None]),
            "sin": bf(np.sin(emb)[None]),
            "Wq": bf(np.random.standard_normal((H * D, HID)) * c / s[None, :]),
            "Wk": bf(np.random.standard_normal((KV * D, HID)) * c / s[None, :]),
            "Wv": bf(np.random.standard_normal((KV * D, HID)) * c / s[None, :]),
            "q_norm_w": bf(0.5 + 0.1 * np.random.standard_normal(D)),
            "k_norm_w": bf(0.5 + 0.1 * np.random.standard_normal(D))}


def reference(hidden_states, cos, sin, Wq, Wk, Wv, q_norm_w, k_norm_w):
    xq = mxq(f64(hidden_states), 2, "e4m3")
    cs = f64(cos)[:, :, None, :]
    sn = f64(sin)[:, :, None, :]
    q = (xq @ mxq(f64(Wq).T, 0, "e4m3")).reshape(B, S, H, D)
    k = (xq @ mxq(f64(Wk).T, 0, "e4m3")).reshape(B, S, KV, D)
    v = (xq @ mxq(f64(Wv).T, 0, "e4m3")).reshape(B, S, KV, D)
    q = rms_norm(q, f64(q_norm_w))
    q = q * cs + rotate_half(q) * sn
    k = rms_norm(k, f64(k_norm_w))
    k = k * cs + rotate_half(k) * sn
    v = rms_norm(v)
    return q.transpose(0, 2, 1, 3), k.transpose(0, 2, 1, 3), v.transpose(0, 2, 1, 3)

@@ -1,0 +1,252 @@
+from contextlib import ExitStack
+
+import concourse.mybir as mybir
+from concourse.masks import make_identity
+
+BF16 = mybir.dt.bfloat16
+F32 = mybir.dt.float32
+U32 = mybir.dt.uint32
+U8 = mybir.dt.uint8
+FP8X4 = mybir.dt.float8_e4m3fn_x4
+ACT = mybir.ActivationFunctionType
+ALU = mybir.AluOpType
+
+P = 128
+PACK = 4
+K_PASS = P * PACK
+
+TOKENS = 4096
+HID = 1024
+D = 128
+HALF = D // 2
+EPS = 1e-6
+HEADS = 4
+ROTATED = 3
+V_HEAD = 3
+FEATURES = HEADS * D
+
+PASSES = HID // K_PASS
+WORDS = HID // 2
+TURNS = WORDS // P
+TILES = TOKENS // P
+TILES_PER_ROUND = 2
+ROUNDS = TILES // TILES_PER_ROUND
+
+FLOPS = 2 * TOKENS * HID * FEATURES
+
+
+def tile_refattention_pa_t_kernel(
+    tc, hidden_states, cos, sin, Wq, Wk, Wv, q_norm_w, k_norm_w, out_0, out_1, out_2
+):
+    nc = tc.nc
+
+    x_view = hidden_states.flatten_outer_dims().rearrange("(p j) k -> p j k", j=TILES)
+    cos_view = cos.flatten_outer_dims().rearrange("(p j) d -> p j d", j=TILES)
+    sin_view = sin.flatten_outer_dims().rearrange("(p j) d -> p j d", j=TILES)
+    q_view = out_0.flatten_outer_dims().rearrange("(h p j) d -> p h j d", h=2, j=TILES)
+    k_view = out_1.flatten_outer_dims().rearrange("(p j) d -> p j d", j=TILES)
+    v_view = out_2.flatten_outer_dims().rearrange("(p j) d -> p j d", j=TILES)
+
+    with ExitStack() as stack:
+        stack.enter_context(tc.manual_schedule())
+        consts = stack.enter_context(tc.tile_pool(name="consts", bufs=1))
+        x_pool = stack.enter_context(tc.tile_pool(name="x", bufs=ROUNDS))
+        stage = stack.enter_context(tc.tile_pool(name="stage", bufs=2))
+        stats = stack.enter_context(tc.tile_pool(name="stats", bufs=3))
+        results = stack.enter_context(tc.tile_pool(name="results", bufs=4))
+        psum_turn = stack.enter_context(tc.psum_pool(name="psum_turn", bufs=2 * TILES_PER_ROUND))
+        psum_prod = stack.enter_context(tc.psum_pool(name="psum_prod", bufs=2 * TILES_PER_ROUND))
+
+        gain_q = consts.tile([P, D], BF16)
+        gain_k = consts.tile([P, D], BF16)
+        nc.scalar.dma_start(out=gain_q[:], in_=q_norm_w.partition_broadcast(P))
+        nc.scalar.dma_start(out=gain_k[:], in_=k_norm_w.partition_broadcast(P))
+        gain_of_head = [gain_q, gain_q, gain_k]
+
+        w_raw = consts.tile([P, HEADS, HID], BF16)
+        nc.sync.dma_start(out=w_raw[:, 0:2, :], in_=Wq.rearrange("(h p) k -> p h k", p=P))
+        nc.sync.dma_start(out=w_raw[:, 2, :], in_=Wk)
+        nc.sync.dma_start(out=w_raw[:, 3, :], in_=Wv)
+
+        cos_sb = consts.tile([P, TILES, D], BF16)
+        sin_sb = consts.tile([P, TILES, D], BF16)
+        x_rounds = []
+        for r in range(ROUNDS):
+            x_sb = x_pool.tile([P, TILES_PER_ROUND, HID], BF16)
+            first = r * TILES_PER_ROUND
+            nc.sync.dma_start(out=x_sb[:], in_=x_view[:, first : first + TILES_PER_ROUND, :])
+            x_rounds.append(x_sb)
+            if r == 1:
+                nc.sync.dma_start(out=cos_sb[:], in_=cos_view)
+                nc.sync.dma_start(out=sin_sb[:], in_=sin_view)
+
+        identity = consts.tile([P, P], F32)
+        make_identity(nc, identity[:])
+        eps = consts.tile([P, 1], F32)
+        nc.vector.memset(eps[:], EPS)
+        table_warmer = consts.tile([P, 1], F32)
+        nc.scalar.activation(out=table_warmer[:], in_=eps[:], func=ACT.Abs_reciprocal_sqrt)
+
+        def turn(rows_as_words):
+            turned = psum_turn.tile([P, TURNS, P], F32)
+            for c in range(TURNS):
+                nc.tensor.transpose(turned[:, c, :], rows_as_words[:, c * P : (c + 1) * P], identity[:])
+            return turned
+
+        def side_by_side(turned):
+            return turned[:].rearrange("p (g u) r -> p g r u", u=2)
+
+        w_grouped = consts.tile([P, PASSES, FEATURES, PACK], BF16, align_bytes=64)
+        w_grouped_words = w_grouped[:].bitcast(F32)
+        w_words = w_raw[:].bitcast(F32)
+        for h in range(HEADS):
+            turned = turn(w_words[:, h, :])
+            copy_out = nc.scalar.copy if h % 2 == 0 else nc.vector.tensor_copy
+            copy_out(out=w_grouped_words[:, :, h * D : (h + 1) * D, :], in_=side_by_side(turned))
+        w_codes = consts.tile([P, PASSES, FEATURES], U32, align_bytes=64)
+        w_scales = consts.tile([P, PASSES, FEATURES], U8, align_bytes=64)
+        for g in range(PASSES):
+            nc.vector.quantize_mx(
+                out=w_codes[:, g, :].bitcast(FP8X4),
+                scales=w_scales[:, g, :],
+                in_=w_grouped[:, g, :, :].rearrange("p f t -> p (f t)"),
+            )
+
+        turned_of = {}
+        grouped_of = {}
+        codes_of = {}
+        product_of = {}
+        rstd_of = {}
+        result_of = {}
+        normed_of = {}
+
+        def transpose_tokens(r):
+            x_words = x_rounds[r][:].bitcast(F32)
+            turned_of[r] = [turn(x_words[:, t, :]) for t in range(TILES_PER_ROUND)]
+
+        def regroup(r):
+            grouped = stage.tile([P, TILES_PER_ROUND, PASSES, P, PACK], BF16, align_bytes=64)
+            grouped_words = grouped[:].bitcast(F32)
+            for t in range(TILES_PER_ROUND):
+                nc.scalar.copy(out=grouped_words[:, t], in_=side_by_side(turned_of[r][t]))
+            grouped_of[r] = grouped
+
+        def quantise(r):
+            codes = stats.tile([P, TILES_PER_ROUND, PASSES, P], U32, align_bytes=64)
+            scales = stats.tile([P, TILES_PER_ROUND, PASSES, P], U8, align_bytes=64)
+            nc.vector.quantize_mx(
+                out=codes[:].rearrange("p t g r -> p (t g r)").bitcast(FP8X4),
+                scales=scales[:].rearrange("p t g r -> p (t g r)"),
+                in_=grouped_of[r][:].rearrange("p t g r v -> p (t g r v)"),
+            )
+            codes_of[r] = (codes, scales)
+
+        def project(r):
+            codes, scales = codes_of[r]
+            product_of[r] = []
+            for t in range(TILES_PER_ROUND):
+                product = psum_prod.tile([P, FEATURES], F32)
+                for g in range(PASSES):
+                    nc.tensor.matmul_mx(
+                        out=product[:],
+                        lhsT=codes[:, t, g, :].bitcast(FP8X4),
+                        lhsT_scale=scales[:, t, g, :],
+                        rhs=w_codes[:, g, :].bitcast(FP8X4),
+                        rhs_scale=w_scales[:, g, :],
+                        start=(g == 0),
+                        stop=(g == PASSES - 1),
+                    )
+                product_of[r].append(product)
+
+        def norm_factors(r):
+            sum_sq = stats.tile([P, HEADS, TILES_PER_ROUND], F32)
+            squares = stage.tile([P, HEADS, TILES_PER_ROUND, D], BF16)
+            for t in range(TILES_PER_ROUND):
+                for h in range(HEADS):
+                    nc.scalar.activation(
+                        out=squares[:, h, t, :],
+                        in_=product_of[r][t][:, h * D : (h + 1) * D],
+                        func=ACT.Square,
+                        accum_out=sum_sq[:, h, t : t + 1],
+                    )
+            rstd_v = stats.tile([P, TILES_PER_ROUND], F32)
+            nc.scalar.activation(
+                out=rstd_v[:], in_=sum_sq[:, V_HEAD, :], func=ACT.Abs_reciprocal_sqrt, scale=1.0 / D, bias=eps[:]
+            )
+            result = results.tile([P, HEADS, TILES_PER_ROUND, D], F32)
+            for t in range(TILES_PER_ROUND):
+                nc.scalar.activation(
+                    out=result[:, V_HEAD, t, :],
+                    in_=product_of[r][t][:, V_HEAD * D : FEATURES],
+                    func=ACT.Copy,
+                    scale=rstd_v[:, t : t + 1],
+                )
+            rstd = stats.tile([P, ROTATED, TILES_PER_ROUND], F32)
+            nc.scalar.activation(
+                out=rstd[:], in_=sum_sq[:, 0:ROTATED, :], func=ACT.Abs_reciprocal_sqrt, scale=1.0 / D, bias=eps[:]
+            )
+            rstd_of[r] = rstd
+            result_of[r] = result
+
+        def normalise(r):
+            normed = stage.tile([P, ROTATED, TILES_PER_ROUND, D], F32)
+            for t in range(TILES_PER_ROUND):
+                for h in range(ROTATED):
+                    nc.vector.scalar_tensor_tensor(
+                        out=normed[:, h, t, :],
+                        in0=product_of[r][t][:, h * D : (h + 1) * D],
+                        scalar=rstd_of[r][:, h, t : t + 1],
+                        in1=gain_of_head[h][:],
+                        op0=ALU.mult,
+                        op1=ALU.mult,
+                    )
+            normed_of[r] = normed
+
+        def rotate_and_store(r):
+            first = r * TILES_PER_ROUND
+            tiles = slice(first, first + TILES_PER_ROUND)
+            low = slice(0, HALF)
+            high = slice(HALF, D)
+            normed = normed_of[r]
+            result = result_of[r]
+
+            def over_heads(table, columns, width):
+                return table[:, tiles, columns].unsqueeze(1).to_broadcast([P, ROTATED, TILES_PER_ROUND, width])
+
+            with_cos = stage.tile([P, ROTATED, TILES_PER_ROUND, D], F32)
+            with_sin = stage.tile([P, ROTATED, TILES_PER_ROUND, D], F32)
+            nc.vector.tensor_tensor(out=with_cos[:], in0=normed[:], in1=over_heads(cos_sb, slice(0, D), D), op=ALU.mult)
+            nc.vector.tensor_tensor(
+                out=with_sin[:, :, :, low], in0=normed[:, :, :, high], in1=over_heads(sin_sb, low, HALF), op=ALU.mult
+            )
+            nc.vector.tensor_tensor(
+                out=with_sin[:, :, :, high], in0=normed[:, :, :, low], in1=over_heads(sin_sb, high, HALF), op=ALU.mult
+            )
+            nc.vector.tensor_tensor(
+                out=result[:, 0:ROTATED, :, low], in0=with_cos[:, :, :, low], in1=with_sin[:, :, :, low], op=ALU.subtract
+            )
+            nc.vector.tensor_tensor(
+                out=result[:, 0:ROTATED, :, high], in0=with_cos[:, :, :, high], in1=with_sin[:, :, :, high], op=ALU.add
+            )
+            nc.sync.dma_start(out=q_view[:, :, tiles, :], in_=result[:, 0:2, :, :])
+            nc.sync.dma_start(out=k_view[:, tiles, :], in_=result[:, 2, :, :])
+            nc.sync.dma_start(out=v_view[:, tiles, :], in_=result[:, V_HEAD, :, :])
+
+        def in_range(r):
+            return 0 <= r < ROUNDS
+
+        for i in range(-3, ROUNDS):
+            if in_range(i + 1):
+                project(i + 1)
+            if in_range(i + 3):
+                transpose_tokens(i + 3)
+            if in_range(i + 2):
+                regroup(i + 2)
+            if in_range(i + 1):
+                norm_factors(i + 1)
+            if in_range(i):
+                normalise(i)
+            if in_range(i + 2):
+                quantise(i + 2)
+            if in_range(i):
+                rotate_and_store(i)

@@ -23,6 +23,9 @@ EPS = 1e-6
 HEADS = 4
 ROTATED = 3
 V_HEAD = 3
+GAINS = 2
+COS = 0
+SIN = 1
 FEATURES = HEADS * D
 
 PASSES = HID // K_PASS
@@ -31,6 +34,7 @@ TURNS = WORDS // P
 TILES = TOKENS // P
 TILES_PER_ROUND = 2
 ROUNDS = TILES // TILES_PER_ROUND
+LOAD_AHEAD = 6
 
 FLOPS = 2 * TOKENS * HID * FEATURES
 
@@ -53,32 +57,37 @@ def tile_refattention_pa_t_kernel(
         x_pool = stack.enter_context(tc.tile_pool(name="x", bufs=ROUNDS))
         stage = stack.enter_context(tc.tile_pool(name="stage", bufs=2))
         stats = stack.enter_context(tc.tile_pool(name="stats", bufs=3))
+        fold = stack.enter_context(tc.tile_pool(name="fold", bufs=3))
         results = stack.enter_context(tc.tile_pool(name="results", bufs=4))
         psum_turn = stack.enter_context(tc.psum_pool(name="psum_turn", bufs=2 * TILES_PER_ROUND))
         psum_prod = stack.enter_context(tc.psum_pool(name="psum_prod", bufs=2 * TILES_PER_ROUND))
 
-        gain_q = consts.tile([P, D], BF16)
-        gain_k = consts.tile([P, D], BF16)
-        nc.scalar.dma_start(out=gain_q[:], in_=q_norm_w.partition_broadcast(P))
-        nc.scalar.dma_start(out=gain_k[:], in_=k_norm_w.partition_broadcast(P))
-        gain_of_head = [gain_q, gain_q, gain_k]
+        gains = consts.tile([P, GAINS, D], BF16)
+        nc.scalar.dma_start(out=gains[:, 0, :], in_=q_norm_w.partition_broadcast(P))
+        nc.scalar.dma_start(out=gains[:, 1, :], in_=k_norm_w.partition_broadcast(P))
+        gain_of_head = [0, 0, 1]
 
         w_raw = consts.tile([P, HEADS, HID], BF16)
         nc.sync.dma_start(out=w_raw[:, 0:2, :], in_=Wq.rearrange("(h p) k -> p h k", p=P))
         nc.sync.dma_start(out=w_raw[:, 2, :], in_=Wk)
         nc.sync.dma_start(out=w_raw[:, 3, :], in_=Wv)
 
-        cos_sb = consts.tile([P, TILES, D], BF16)
-        sin_sb = consts.tile([P, TILES, D], BF16)
-        x_rounds = []
-        for r in range(ROUNDS):
-            x_sb = x_pool.tile([P, TILES_PER_ROUND, HID], BF16)
+        x_of = {}
+        tables_of = {}
+
+        def load_tokens(r):
             first = r * TILES_PER_ROUND
-            nc.sync.dma_start(out=x_sb[:], in_=x_view[:, first : first + TILES_PER_ROUND, :])
-            x_rounds.append(x_sb)
-            if r == 1:
-                nc.sync.dma_start(out=cos_sb[:], in_=cos_view)
-                nc.sync.dma_start(out=sin_sb[:], in_=sin_view)
+            tiles = slice(first, first + TILES_PER_ROUND)
+            x_sb = x_pool.tile([P, TILES_PER_ROUND, HID], BF16)
+            nc.sync.dma_start(out=x_sb[:], in_=x_view[:, tiles, :])
+            tables = x_pool.tile([P, 2, TILES_PER_ROUND, D], BF16)
+            nc.sync.dma_start(out=tables[:, COS, :, :], in_=cos_view[:, tiles, :])
+            nc.sync.dma_start(out=tables[:, SIN, :, :], in_=sin_view[:, tiles, :])
+            x_of[r] = x_sb
+            tables_of[r] = tables
+
+        for r in range(LOAD_AHEAD - 3):
+            load_tokens(r)
 
         identity = consts.tile([P, P], F32)
         make_identity(nc, identity[:])
@@ -118,10 +127,11 @@ def tile_refattention_pa_t_kernel(
         product_of = {}
         rstd_of = {}
         result_of = {}
-        normed_of = {}
+        folded_of = {}
+        scaled_of = {}
 
         def transpose_tokens(r):
-            x_words = x_rounds[r][:].bitcast(F32)
+            x_words = x_of[r][:].bitcast(F32)
             turned_of[r] = [turn(x_words[:, t, :]) for t in range(TILES_PER_ROUND)]
 
         def regroup(r):
@@ -188,45 +198,56 @@ def tile_refattention_pa_t_kernel(
             rstd_of[r] = rstd
             result_of[r] = result
 
-        def normalise(r):
-            normed = stage.tile([P, ROTATED, TILES_PER_ROUND, D], F32)
+        low = slice(0, HALF)
+        high = slice(HALF, D)
+
+        def fold_gains(r):
+            tables = tables_of[r]
+            folded = fold.tile([P, 2, GAINS, TILES_PER_ROUND, D], F32)
+
+            def over_gains(table, columns, width):
+                return tables[:, table, :, columns].unsqueeze(1).to_broadcast([P, GAINS, TILES_PER_ROUND, width])
+
+            def over_tiles(columns, width):
+                return gains[:, :, columns].unsqueeze(2).to_broadcast([P, GAINS, TILES_PER_ROUND, width])
+
+            whole = slice(0, D)
+            nc.gpsimd.tensor_tensor(
+                out=folded[:, COS, :, :, :], in0=over_gains(COS, whole, D), in1=over_tiles(whole, D), op=ALU.mult
+            )
+            nc.gpsimd.tensor_tensor(
+                out=folded[:, SIN, :, :, low], in0=over_gains(SIN, high, HALF), in1=over_tiles(low, HALF), op=ALU.mult
+            )
+            nc.gpsimd.tensor_tensor(
+                out=folded[:, SIN, :, :, high], in0=over_gains(SIN, low, HALF), in1=over_tiles(high, HALF), op=ALU.mult
+            )
+            folded_of[r] = folded
+
+        def scale_by_tables(r):
+            scaled = stage.tile([P, 2, ROTATED, TILES_PER_ROUND, D], F32)
             for t in range(TILES_PER_ROUND):
                 for h in range(ROTATED):
-                    nc.vector.scalar_tensor_tensor(
-                        out=normed[:, h, t, :],
-                        in0=product_of[r][t][:, h * D : (h + 1) * D],
-                        scalar=rstd_of[r][:, h, t : t + 1],
-                        in1=gain_of_head[h][:],
-                        op0=ALU.mult,
-                        op1=ALU.mult,
-                    )
-            normed_of[r] = normed
+                    for table in (COS, SIN):
+                        nc.vector.scalar_tensor_tensor(
+                            out=scaled[:, table, h, t, :],
+                            in0=product_of[r][t][:, h * D : (h + 1) * D],
+                            scalar=rstd_of[r][:, h, t : t + 1],
+                            in1=folded_of[r][:, table, gain_of_head[h], t, :],
+                            op0=ALU.mult,
+                            op1=ALU.mult,
+                        )
+            scaled_of[r] = scaled
 
-        def rotate_and_store(r):
+        def join_and_store(r):
+            scaled = scaled_of[r]
             first = r * TILES_PER_ROUND
             tiles = slice(first, first + TILES_PER_ROUND)
-            low = slice(0, HALF)
-            high = slice(HALF, D)
-            normed = normed_of[r]
             result = result_of[r]
-
-            def over_heads(table, columns, width):
-                return table[:, tiles, columns].unsqueeze(1).to_broadcast([P, ROTATED, TILES_PER_ROUND, width])
-
-            with_cos = stage.tile([P, ROTATED, TILES_PER_ROUND, D], F32)
-            with_sin = stage.tile([P, ROTATED, TILES_PER_ROUND, D], F32)
-            nc.vector.tensor_tensor(out=with_cos[:], in0=normed[:], in1=over_heads(cos_sb, slice(0, D), D), op=ALU.mult)
             nc.vector.tensor_tensor(
-                out=with_sin[:, :, :, low], in0=normed[:, :, :, high], in1=over_heads(sin_sb, low, HALF), op=ALU.mult
+                out=result[:, 0:ROTATED, :, low], in0=scaled[:, COS, :, :, low], in1=scaled[:, SIN, :, :, high], op=ALU.subtract
             )
             nc.vector.tensor_tensor(
-                out=with_sin[:, :, :, high], in0=normed[:, :, :, low], in1=over_heads(sin_sb, high, HALF), op=ALU.mult
-            )
-            nc.vector.tensor_tensor(
-                out=result[:, 0:ROTATED, :, low], in0=with_cos[:, :, :, low], in1=with_sin[:, :, :, low], op=ALU.subtract
-            )
-            nc.vector.tensor_tensor(
-                out=result[:, 0:ROTATED, :, high], in0=with_cos[:, :, :, high], in1=with_sin[:, :, :, high], op=ALU.add
+                out=result[:, 0:ROTATED, :, high], in0=scaled[:, COS, :, :, high], in1=scaled[:, SIN, :, :, low], op=ALU.add
             )
             nc.sync.dma_start(out=q_view[:, :, tiles, :], in_=result[:, 0:2, :, :])
             nc.sync.dma_start(out=k_view[:, tiles, :], in_=result[:, 2, :, :])
@@ -236,6 +257,8 @@ def tile_refattention_pa_t_kernel(
             return 0 <= r < ROUNDS
 
         for i in range(-3, ROUNDS):
+            if in_range(i + LOAD_AHEAD):
+                load_tokens(i + LOAD_AHEAD)
             if in_range(i + 1):
                 project(i + 1)
             if in_range(i + 3):
@@ -244,9 +267,11 @@ def tile_refattention_pa_t_kernel(
                 regroup(i + 2)
             if in_range(i + 1):
                 norm_factors(i + 1)
+            if in_range(i + 2):
+                fold_gains(i + 2)
             if in_range(i):
-                normalise(i)
+                scale_by_tables(i)
             if in_range(i + 2):
                 quantise(i + 2)
             if in_range(i):
-                rotate_and_store(i)
+                join_and_store(i)

@@ -22,8 +22,9 @@ HALF = D // 2
 EPS = 1e-6
 HEADS = 4
 ROTATED = 3
+Q_HEADS = 2
+K_HEAD = 2
 V_HEAD = 3
-GAINS = 2
 COS = 0
 SIN = 1
 FEATURES = HEADS * D
@@ -62,15 +63,14 @@ def tile_refattention_pa_t_kernel(
         psum_turn = stack.enter_context(tc.psum_pool(name="psum_turn", bufs=2 * TILES_PER_ROUND))
         psum_prod = stack.enter_context(tc.psum_pool(name="psum_prod", bufs=2 * TILES_PER_ROUND))
 
-        gains = consts.tile([P, GAINS, D], BF16)
-        nc.scalar.dma_start(out=gains[:, 0, :], in_=q_norm_w.partition_broadcast(P))
-        nc.scalar.dma_start(out=gains[:, 1, :], in_=k_norm_w.partition_broadcast(P))
-        gain_of_head = [0, 0, 1]
+        gain_q = consts.tile([P, D], BF16)
+        gain_k = consts.tile([P, D], BF16)
+        nc.scalar.dma_start(out=gain_q[:], in_=q_norm_w.partition_broadcast(P))
+        nc.scalar.dma_start(out=gain_k[:], in_=k_norm_w.partition_broadcast(P))
 
         w_raw = consts.tile([P, HEADS, HID], BF16)
-        nc.sync.dma_start(out=w_raw[:, 0:2, :], in_=Wq.rearrange("(h p) k -> p h k", p=P))
-        nc.sync.dma_start(out=w_raw[:, 2, :], in_=Wk)
-        nc.sync.dma_start(out=w_raw[:, 3, :], in_=Wv)
+        for h, rows in enumerate((Wq[0:D, :], Wq[D : 2 * D, :], Wk, Wv)):
+            nc.sync.dma_start(out=w_raw[:, h, :], in_=rows)
 
         x_of = {}
         tables_of = {}
@@ -128,7 +128,8 @@ def tile_refattention_pa_t_kernel(
         rstd_of = {}
         result_of = {}
         folded_of = {}
-        scaled_of = {}
+        terms_of = {}
+        normed_of = {}
 
         def transpose_tokens(r):
             x_words = x_of[r][:].bitcast(F32)
@@ -171,18 +172,25 @@ def tile_refattention_pa_t_kernel(
         def norm_factors(r):
             sum_sq = stats.tile([P, HEADS, TILES_PER_ROUND], F32)
             squares = stage.tile([P, HEADS, TILES_PER_ROUND, D], BF16)
-            for t in range(TILES_PER_ROUND):
-                for h in range(HEADS):
-                    nc.scalar.activation(
-                        out=squares[:, h, t, :],
-                        in_=product_of[r][t][:, h * D : (h + 1) * D],
-                        func=ACT.Square,
-                        accum_out=sum_sq[:, h, t : t + 1],
-                    )
+
+            def sum_squares(t, h):
+                nc.scalar.activation(
+                    out=squares[:, h, t, :],
+                    in_=product_of[r][t][:, h * D : (h + 1) * D],
+                    func=ACT.Square,
+                    accum_out=sum_sq[:, h, t : t + 1],
+                )
+
+            def reciprocal_rms(out, sums):
+                nc.scalar.activation(out=out, in_=sums, func=ACT.Abs_reciprocal_sqrt, scale=1.0 / D, bias=eps[:])
+
+            sums_in_order = [(t, h) for t in range(TILES_PER_ROUND) for h in (V_HEAD, 0, 1, 2)]
+            for t, h in sums_in_order[:-2]:
+                sum_squares(t, h)
             rstd_v = stats.tile([P, TILES_PER_ROUND], F32)
-            nc.scalar.activation(
-                out=rstd_v[:], in_=sum_sq[:, V_HEAD, :], func=ACT.Abs_reciprocal_sqrt, scale=1.0 / D, bias=eps[:]
-            )
+            reciprocal_rms(rstd_v[:], sum_sq[:, V_HEAD, :])
+            for t, h in sums_in_order[-2:]:
+                sum_squares(t, h)
             result = results.tile([P, HEADS, TILES_PER_ROUND, D], F32)
             for t in range(TILES_PER_ROUND):
                 nc.scalar.activation(
@@ -192,65 +200,72 @@ def tile_refattention_pa_t_kernel(
                     scale=rstd_v[:, t : t + 1],
                 )
             rstd = stats.tile([P, ROTATED, TILES_PER_ROUND], F32)
-            nc.scalar.activation(
-                out=rstd[:], in_=sum_sq[:, 0:ROTATED, :], func=ACT.Abs_reciprocal_sqrt, scale=1.0 / D, bias=eps[:]
-            )
+            reciprocal_rms(rstd[:], sum_sq[:, 0:ROTATED, :])
             rstd_of[r] = rstd
             result_of[r] = result
 
         low = slice(0, HALF)
         high = slice(HALF, D)
+        other_half = ((high, low), (low, high))
 
-        def fold_gains(r):
+        def over_tiles(gain, columns, width):
+            return gain[:, columns].unsqueeze(1).to_broadcast([P, TILES_PER_ROUND, width])
+
+        def fold_q_gain(r):
             tables = tables_of[r]
-            folded = fold.tile([P, 2, GAINS, TILES_PER_ROUND, D], F32)
-
-            def over_gains(table, columns, width):
-                return tables[:, table, :, columns].unsqueeze(1).to_broadcast([P, GAINS, TILES_PER_ROUND, width])
-
-            def over_tiles(columns, width):
-                return gains[:, :, columns].unsqueeze(2).to_broadcast([P, GAINS, TILES_PER_ROUND, width])
-
-            whole = slice(0, D)
+            folded = fold.tile([P, 2, TILES_PER_ROUND, D], F32)
             nc.gpsimd.tensor_tensor(
-                out=folded[:, COS, :, :, :], in0=over_gains(COS, whole, D), in1=over_tiles(whole, D), op=ALU.mult
+                out=folded[:, COS, :, :], in0=tables[:, COS, :, :], in1=over_tiles(gain_q, slice(0, D), D), op=ALU.mult
             )
-            nc.gpsimd.tensor_tensor(
-                out=folded[:, SIN, :, :, low], in0=over_gains(SIN, high, HALF), in1=over_tiles(low, HALF), op=ALU.mult
-            )
-            nc.gpsimd.tensor_tensor(
-                out=folded[:, SIN, :, :, high], in0=over_gains(SIN, low, HALF), in1=over_tiles(high, HALF), op=ALU.mult
-            )
+            for here, there in other_half:
+                nc.gpsimd.tensor_tensor(
+                    out=folded[:, SIN, :, here], in0=tables[:, SIN, :, there], in1=over_tiles(gain_q, here, HALF), op=ALU.mult
+                )
             folded_of[r] = folded
 
-        def scale_by_tables(r):
-            scaled = stage.tile([P, 2, ROTATED, TILES_PER_ROUND, D], F32)
-            for t in range(TILES_PER_ROUND):
-                for h in range(ROTATED):
-                    for table in (COS, SIN):
-                        nc.vector.scalar_tensor_tensor(
-                            out=scaled[:, table, h, t, :],
-                            in0=product_of[r][t][:, h * D : (h + 1) * D],
-                            scalar=rstd_of[r][:, h, t : t + 1],
-                            in1=folded_of[r][:, table, gain_of_head[h], t, :],
-                            op0=ALU.mult,
-                            op1=ALU.mult,
-                        )
-            scaled_of[r] = scaled
+        def scale_products(r):
+            normed_k = stage.tile([P, TILES_PER_ROUND, D], F32)
+            terms = stage.tile([P, 2, ROTATED, TILES_PER_ROUND, D], F32)
 
-        def join_and_store(r):
-            scaled = scaled_of[r]
+            def times_rstd_times(out, t, h, in1):
+                nc.vector.scalar_tensor_tensor(
+                    out=out,
+                    in0=product_of[r][t][:, h * D : (h + 1) * D],
+                    scalar=rstd_of[r][:, h, t : t + 1],
+                    in1=in1,
+                    op0=ALU.mult,
+                    op1=ALU.mult,
+                )
+
+            for t in range(TILES_PER_ROUND):
+                times_rstd_times(normed_k[:, t, :], t, K_HEAD, gain_k[:])
+            for t in range(TILES_PER_ROUND):
+                for h in range(Q_HEADS):
+                    for table in (COS, SIN):
+                        times_rstd_times(terms[:, table, h, t, :], t, h, folded_of[r][:, table, t, :])
+            normed_of[r] = normed_k
+            terms_of[r] = terms
+
+        def rotate_and_store(r):
             first = r * TILES_PER_ROUND
             tiles = slice(first, first + TILES_PER_ROUND)
+            tables = tables_of[r]
+            normed_k = normed_of[r]
+            terms = terms_of[r]
             result = result_of[r]
+            nc.vector.tensor_tensor(out=terms[:, COS, K_HEAD, :, :], in0=normed_k[:], in1=tables[:, COS, :, :], op=ALU.mult)
+            for here, there in other_half:
+                nc.vector.tensor_tensor(
+                    out=terms[:, SIN, K_HEAD, :, here], in0=normed_k[:, :, here], in1=tables[:, SIN, :, there], op=ALU.mult
+                )
             nc.vector.tensor_tensor(
-                out=result[:, 0:ROTATED, :, low], in0=scaled[:, COS, :, :, low], in1=scaled[:, SIN, :, :, high], op=ALU.subtract
+                out=result[:, 0:ROTATED, :, low], in0=terms[:, COS, :, :, low], in1=terms[:, SIN, :, :, high], op=ALU.subtract
             )
             nc.vector.tensor_tensor(
-                out=result[:, 0:ROTATED, :, high], in0=scaled[:, COS, :, :, high], in1=scaled[:, SIN, :, :, low], op=ALU.add
+                out=result[:, 0:ROTATED, :, high], in0=terms[:, COS, :, :, high], in1=terms[:, SIN, :, :, low], op=ALU.add
             )
-            nc.sync.dma_start(out=q_view[:, :, tiles, :], in_=result[:, 0:2, :, :])
-            nc.sync.dma_start(out=k_view[:, tiles, :], in_=result[:, 2, :, :])
+            nc.sync.dma_start(out=q_view[:, :, tiles, :], in_=result[:, 0:Q_HEADS, :, :])
+            nc.sync.dma_start(out=k_view[:, tiles, :], in_=result[:, K_HEAD, :, :])
             nc.sync.dma_start(out=v_view[:, tiles, :], in_=result[:, V_HEAD, :, :])
 
         def in_range(r):
@@ -268,10 +283,10 @@ def tile_refattention_pa_t_kernel(
             if in_range(i + 1):
                 norm_factors(i + 1)
             if in_range(i + 2):
-                fold_gains(i + 2)
+                fold_q_gain(i + 2)
             if in_range(i):
-                scale_by_tables(i)
+                scale_products(i)
             if in_range(i + 2):
                 quantise(i + 2)
             if in_range(i):
-                join_and_store(i)
+                rotate_and_store(i)

@@ -22,11 +22,7 @@ HALF = D // 2
 EPS = 1e-6
 HEADS = 4
 ROTATED = 3
-Q_HEADS = 2
-K_HEAD = 2
 V_HEAD = 3
-COS = 0
-SIN = 1
 FEATURES = HEADS * D
 
 PASSES = HID // K_PASS
@@ -58,7 +54,6 @@ def tile_refattention_pa_t_kernel(
         x_pool = stack.enter_context(tc.tile_pool(name="x", bufs=ROUNDS))
         stage = stack.enter_context(tc.tile_pool(name="stage", bufs=2))
         stats = stack.enter_context(tc.tile_pool(name="stats", bufs=3))
-        fold = stack.enter_context(tc.tile_pool(name="fold", bufs=3))
         results = stack.enter_context(tc.tile_pool(name="results", bufs=4))
         psum_turn = stack.enter_context(tc.psum_pool(name="psum_turn", bufs=2 * TILES_PER_ROUND))
         psum_prod = stack.enter_context(tc.psum_pool(name="psum_prod", bufs=2 * TILES_PER_ROUND))
@@ -67,27 +62,27 @@ def tile_refattention_pa_t_kernel(
         gain_k = consts.tile([P, D], BF16)
         nc.scalar.dma_start(out=gain_q[:], in_=q_norm_w.partition_broadcast(P))
         nc.scalar.dma_start(out=gain_k[:], in_=k_norm_w.partition_broadcast(P))
+        gain_of_head = [gain_q, gain_q, gain_k]
 
         w_raw = consts.tile([P, HEADS, HID], BF16)
         for h, rows in enumerate((Wq[0:D, :], Wq[D : 2 * D, :], Wk, Wv)):
             nc.sync.dma_start(out=w_raw[:, h, :], in_=rows)
 
         x_of = {}
-        tables_of = {}
 
         def load_tokens(r):
-            first = r * TILES_PER_ROUND
-            tiles = slice(first, first + TILES_PER_ROUND)
             x_sb = x_pool.tile([P, TILES_PER_ROUND, HID], BF16)
-            nc.sync.dma_start(out=x_sb[:], in_=x_view[:, tiles, :])
-            tables = x_pool.tile([P, 2, TILES_PER_ROUND, D], BF16)
-            nc.sync.dma_start(out=tables[:, COS, :, :], in_=cos_view[:, tiles, :])
-            nc.sync.dma_start(out=tables[:, SIN, :, :], in_=sin_view[:, tiles, :])
+            first = r * TILES_PER_ROUND
+            nc.sync.dma_start(out=x_sb[:], in_=x_view[:, first : first + TILES_PER_ROUND, :])
             x_of[r] = x_sb
-            tables_of[r] = tables
 
-        for r in range(LOAD_AHEAD - 3):
-            load_tokens(r)
+        cos_sb = consts.tile([P, TILES, D], BF16)
+        sin_sb = consts.tile([P, TILES, D], BF16)
+        load_tokens(0)
+        load_tokens(1)
+        nc.sync.dma_start(out=cos_sb[:], in_=cos_view)
+        nc.sync.dma_start(out=sin_sb[:], in_=sin_view)
+        load_tokens(2)
 
         identity = consts.tile([P, P], F32)
         make_identity(nc, identity[:])
@@ -125,10 +120,8 @@ def tile_refattention_pa_t_kernel(
         grouped_of = {}
         codes_of = {}
         product_of = {}
-        rstd_of = {}
+        factors_of = {}
         result_of = {}
-        folded_of = {}
-        terms_of = {}
         normed_of = {}
 
         def transpose_tokens(r):
@@ -192,6 +185,7 @@ def tile_refattention_pa_t_kernel(
             for t, h in sums_in_order[-2:]:
                 sum_squares(t, h)
             result = results.tile([P, HEADS, TILES_PER_ROUND, D], F32)
+            rstd = stats.tile([P, ROTATED, TILES_PER_ROUND], F32)
             for t in range(TILES_PER_ROUND):
                 nc.scalar.activation(
                     out=result[:, V_HEAD, t, :],
@@ -199,73 +193,55 @@ def tile_refattention_pa_t_kernel(
                     func=ACT.Copy,
                     scale=rstd_v[:, t : t + 1],
                 )
-            rstd = stats.tile([P, ROTATED, TILES_PER_ROUND], F32)
-            reciprocal_rms(rstd[:], sum_sq[:, 0:ROTATED, :])
-            rstd_of[r] = rstd
+                if t == 0:
+                    reciprocal_rms(rstd[:], sum_sq[:, 0:ROTATED, :])
+            factors = stage.tile([P, ROTATED, TILES_PER_ROUND, D], F32)
+            for t in range(TILES_PER_ROUND):
+                for h in range(ROTATED):
+                    nc.scalar.activation(
+                        out=factors[:, h, t, :], in_=gain_of_head[h][:], func=ACT.Copy, scale=rstd[:, h, t : t + 1]
+                    )
+            factors_of[r] = factors
             result_of[r] = result
-
-        low = slice(0, HALF)
-        high = slice(HALF, D)
-        other_half = ((high, low), (low, high))
-
-        def over_tiles(gain, columns, width):
-            return gain[:, columns].unsqueeze(1).to_broadcast([P, TILES_PER_ROUND, width])
-
-        def fold_q_gain(r):
-            tables = tables_of[r]
-            folded = fold.tile([P, 2, TILES_PER_ROUND, D], F32)
-            nc.gpsimd.tensor_tensor(
-                out=folded[:, COS, :, :], in0=tables[:, COS, :, :], in1=over_tiles(gain_q, slice(0, D), D), op=ALU.mult
-            )
-            for here, there in other_half:
-                nc.gpsimd.tensor_tensor(
-                    out=folded[:, SIN, :, here], in0=tables[:, SIN, :, there], in1=over_tiles(gain_q, here, HALF), op=ALU.mult
-                )
-            folded_of[r] = folded
-
-        def scale_products(r):
-            normed_k = stage.tile([P, TILES_PER_ROUND, D], F32)
-            terms = stage.tile([P, 2, ROTATED, TILES_PER_ROUND, D], F32)
-
-            def times_rstd_times(out, t, h, in1):
-                nc.vector.scalar_tensor_tensor(
-                    out=out,
-                    in0=product_of[r][t][:, h * D : (h + 1) * D],
-                    scalar=rstd_of[r][:, h, t : t + 1],
-                    in1=in1,
-                    op0=ALU.mult,
-                    op1=ALU.mult,
-                )
-
+        def normalise(r):
+            normed = stage.tile([P, ROTATED, TILES_PER_ROUND, D], F32)
             for t in range(TILES_PER_ROUND):
-                times_rstd_times(normed_k[:, t, :], t, K_HEAD, gain_k[:])
-            for t in range(TILES_PER_ROUND):
-                for h in range(Q_HEADS):
-                    for table in (COS, SIN):
-                        times_rstd_times(terms[:, table, h, t, :], t, h, folded_of[r][:, table, t, :])
-            normed_of[r] = normed_k
-            terms_of[r] = terms
+                nc.vector.tensor_tensor(
+                    out=normed[:, :, t, :],
+                    in0=product_of[r][t][:, 0 : ROTATED * D].rearrange("p (h d) -> p h d", d=D),
+                    in1=factors_of[r][:, :, t, :],
+                    op=ALU.mult,
+                )
+            normed_of[r] = normed
 
         def rotate_and_store(r):
             first = r * TILES_PER_ROUND
             tiles = slice(first, first + TILES_PER_ROUND)
-            tables = tables_of[r]
-            normed_k = normed_of[r]
-            terms = terms_of[r]
+            low = slice(0, HALF)
+            high = slice(HALF, D)
+            normed = normed_of[r]
             result = result_of[r]
-            nc.vector.tensor_tensor(out=terms[:, COS, K_HEAD, :, :], in0=normed_k[:], in1=tables[:, COS, :, :], op=ALU.mult)
-            for here, there in other_half:
-                nc.vector.tensor_tensor(
-                    out=terms[:, SIN, K_HEAD, :, here], in0=normed_k[:, :, here], in1=tables[:, SIN, :, there], op=ALU.mult
-                )
+
+            def over_heads(table, columns, width):
+                return table[:, tiles, columns].unsqueeze(1).to_broadcast([P, ROTATED, TILES_PER_ROUND, width])
+
+            with_cos = stage.tile([P, ROTATED, TILES_PER_ROUND, D], F32)
+            with_sin = stage.tile([P, ROTATED, TILES_PER_ROUND, D], F32)
+            nc.vector.tensor_tensor(out=with_cos[:], in0=normed[:], in1=over_heads(cos_sb, slice(0, D), D), op=ALU.mult)
             nc.vector.tensor_tensor(
-                out=result[:, 0:ROTATED, :, low], in0=terms[:, COS, :, :, low], in1=terms[:, SIN, :, :, high], op=ALU.subtract
+                out=with_sin[:, :, :, low], in0=normed[:, :, :, high], in1=over_heads(sin_sb, low, HALF), op=ALU.mult
             )
             nc.vector.tensor_tensor(
-                out=result[:, 0:ROTATED, :, high], in0=terms[:, COS, :, :, high], in1=terms[:, SIN, :, :, low], op=ALU.add
+                out=with_sin[:, :, :, high], in0=normed[:, :, :, low], in1=over_heads(sin_sb, high, HALF), op=ALU.mult
             )
-            nc.sync.dma_start(out=q_view[:, :, tiles, :], in_=result[:, 0:Q_HEADS, :, :])
-            nc.sync.dma_start(out=k_view[:, tiles, :], in_=result[:, K_HEAD, :, :])
+            nc.vector.tensor_tensor(
+                out=result[:, 0:ROTATED, :, low], in0=with_cos[:, :, :, low], in1=with_sin[:, :, :, low], op=ALU.subtract
+            )
+            nc.vector.tensor_tensor(
+                out=result[:, 0:ROTATED, :, high], in0=with_cos[:, :, :, high], in1=with_sin[:, :, :, high], op=ALU.add
+            )
+            nc.sync.dma_start(out=q_view[:, :, tiles, :], in_=result[:, 0:2, :, :])
+            nc.sync.dma_start(out=k_view[:, tiles, :], in_=result[:, 2, :, :])
             nc.sync.dma_start(out=v_view[:, tiles, :], in_=result[:, V_HEAD, :, :])
 
         def in_range(r):
@@ -282,10 +258,8 @@ def tile_refattention_pa_t_kernel(
                 regroup(i + 2)
             if in_range(i + 1):
                 norm_factors(i + 1)
-            if in_range(i + 2):
-                fold_q_gain(i + 2)
             if in_range(i):
-                scale_products(i)
+                normalise(i)
             if in_range(i + 2):
                 quantise(i + 2)
             if in_range(i):

@@ -23,6 +23,9 @@ EPS = 1e-6
 HEADS = 4
 ROTATED = 3
 V_HEAD = 3
+GAINS = 2
+COS = 0
+SIN = 1
 FEATURES = HEADS * D
 
 PASSES = HID // K_PASS
@@ -54,35 +57,37 @@ def tile_refattention_pa_t_kernel(
         x_pool = stack.enter_context(tc.tile_pool(name="x", bufs=ROUNDS))
         stage = stack.enter_context(tc.tile_pool(name="stage", bufs=2))
         stats = stack.enter_context(tc.tile_pool(name="stats", bufs=3))
+        fold = stack.enter_context(tc.tile_pool(name="fold", bufs=3))
         results = stack.enter_context(tc.tile_pool(name="results", bufs=4))
         psum_turn = stack.enter_context(tc.psum_pool(name="psum_turn", bufs=2 * TILES_PER_ROUND))
         psum_prod = stack.enter_context(tc.psum_pool(name="psum_prod", bufs=2 * TILES_PER_ROUND))
 
-        gain_q = consts.tile([P, D], BF16)
-        gain_k = consts.tile([P, D], BF16)
-        nc.scalar.dma_start(out=gain_q[:], in_=q_norm_w.partition_broadcast(P))
-        nc.scalar.dma_start(out=gain_k[:], in_=k_norm_w.partition_broadcast(P))
-        gain_of_head = [gain_q, gain_q, gain_k]
+        gains = consts.tile([P, GAINS, D], BF16)
+        nc.scalar.dma_start(out=gains[:, 0, :], in_=q_norm_w.partition_broadcast(P))
+        nc.scalar.dma_start(out=gains[:, 1, :], in_=k_norm_w.partition_broadcast(P))
+        gain_of_head = [0, 0, 1]
 
         w_raw = consts.tile([P, HEADS, HID], BF16)
-        for h, rows in enumerate((Wq[0:D, :], Wq[D : 2 * D, :], Wk, Wv)):
-            nc.sync.dma_start(out=w_raw[:, h, :], in_=rows)
+        nc.sync.dma_start(out=w_raw[:, 0:2, :], in_=Wq.rearrange("(h p) k -> p h k", p=P))
+        nc.sync.dma_start(out=w_raw[:, 2, :], in_=Wk)
+        nc.sync.dma_start(out=w_raw[:, 3, :], in_=Wv)
 
         x_of = {}
+        tables_of = {}
 
         def load_tokens(r):
-            x_sb = x_pool.tile([P, TILES_PER_ROUND, HID], BF16)
             first = r * TILES_PER_ROUND
-            nc.sync.dma_start(out=x_sb[:], in_=x_view[:, first : first + TILES_PER_ROUND, :])
+            tiles = slice(first, first + TILES_PER_ROUND)
+            x_sb = x_pool.tile([P, TILES_PER_ROUND, HID], BF16)
+            nc.sync.dma_start(out=x_sb[:], in_=x_view[:, tiles, :])
+            tables = x_pool.tile([P, 2, TILES_PER_ROUND, D], BF16)
+            nc.sync.dma_start(out=tables[:, COS, :, :], in_=cos_view[:, tiles, :])
+            nc.sync.dma_start(out=tables[:, SIN, :, :], in_=sin_view[:, tiles, :])
             x_of[r] = x_sb
+            tables_of[r] = tables
 
-        cos_sb = consts.tile([P, TILES, D], BF16)
-        sin_sb = consts.tile([P, TILES, D], BF16)
-        load_tokens(0)
-        load_tokens(1)
-        nc.sync.dma_start(out=cos_sb[:], in_=cos_view)
-        nc.sync.dma_start(out=sin_sb[:], in_=sin_view)
-        load_tokens(2)
+        for r in range(LOAD_AHEAD - 3):
+            load_tokens(r)
 
         identity = consts.tile([P, P], F32)
         make_identity(nc, identity[:])
@@ -120,9 +125,10 @@ def tile_refattention_pa_t_kernel(
         grouped_of = {}
         codes_of = {}
         product_of = {}
-        factors_of = {}
+        rstd_of = {}
         result_of = {}
-        normed_of = {}
+        folded_of = {}
+        scaled_of = {}
 
         def transpose_tokens(r):
             x_words = x_of[r][:].bitcast(F32)
@@ -150,42 +156,35 @@ def tile_refattention_pa_t_kernel(
             product_of[r] = []
             for t in range(TILES_PER_ROUND):
                 product = psum_prod.tile([P, FEATURES], F32)
-                for g in range(PASSES):
-                    nc.tensor.matmul_mx(
-                        out=product[:],
-                        lhsT=codes[:, t, g, :].bitcast(FP8X4),
-                        lhsT_scale=scales[:, t, g, :],
-                        rhs=w_codes[:, g, :].bitcast(FP8X4),
-                        rhs_scale=w_scales[:, g, :],
-                        start=(g == 0),
-                        stop=(g == PASSES - 1),
-                    )
+                for repeat in range(2):
+                    for g in range(PASSES):
+                        nc.tensor.matmul_mx(
+                            out=product[:],
+                            lhsT=codes[:, t, g, :].bitcast(FP8X4),
+                            lhsT_scale=scales[:, t, g, :],
+                            rhs=w_codes[:, g, :].bitcast(FP8X4),
+                            rhs_scale=w_scales[:, g, :],
+                            start=(g == 0),
+                            stop=(g == PASSES - 1),
+                        )
                 product_of[r].append(product)
 
         def norm_factors(r):
             sum_sq = stats.tile([P, HEADS, TILES_PER_ROUND], F32)
             squares = stage.tile([P, HEADS, TILES_PER_ROUND, D], BF16)
-
-            def sum_squares(t, h):
-                nc.scalar.activation(
-                    out=squares[:, h, t, :],
-                    in_=product_of[r][t][:, h * D : (h + 1) * D],
-                    func=ACT.Square,
-                    accum_out=sum_sq[:, h, t : t + 1],
-                )
-
-            def reciprocal_rms(out, sums):
-                nc.scalar.activation(out=out, in_=sums, func=ACT.Abs_reciprocal_sqrt, scale=1.0 / D, bias=eps[:])
-
-            sums_in_order = [(t, h) for t in range(TILES_PER_ROUND) for h in (V_HEAD, 0, 1, 2)]
-            for t, h in sums_in_order[:-2]:
-                sum_squares(t, h)
+            for t in range(TILES_PER_ROUND):
+                for h in range(HEADS):
+                    nc.scalar.activation(
+                        out=squares[:, h, t, :],
+                        in_=product_of[r][t][:, h * D : (h + 1) * D],
+                        func=ACT.Square,
+                        accum_out=sum_sq[:, h, t : t + 1],
+                    )
             rstd_v = stats.tile([P, TILES_PER_ROUND], F32)
-            reciprocal_rms(rstd_v[:], sum_sq[:, V_HEAD, :])
-            for t, h in sums_in_order[-2:]:
-                sum_squares(t, h)
+            nc.scalar.activation(
+                out=rstd_v[:], in_=sum_sq[:, V_HEAD, :], func=ACT.Abs_reciprocal_sqrt, scale=1.0 / D, bias=eps[:]
+            )
             result = results.tile([P, HEADS, TILES_PER_ROUND, D], F32)
-            rstd = stats.tile([P, ROTATED, TILES_PER_ROUND], F32)
             for t in range(TILES_PER_ROUND):
                 nc.scalar.activation(
                     out=result[:, V_HEAD, t, :],
@@ -193,52 +192,63 @@ def tile_refattention_pa_t_kernel(
                     func=ACT.Copy,
                     scale=rstd_v[:, t : t + 1],
                 )
-                if t == 0:
-                    reciprocal_rms(rstd[:], sum_sq[:, 0:ROTATED, :])
-            factors = stage.tile([P, ROTATED, TILES_PER_ROUND, D], F32)
+            rstd = stats.tile([P, ROTATED, TILES_PER_ROUND], F32)
+            nc.scalar.activation(
+                out=rstd[:], in_=sum_sq[:, 0:ROTATED, :], func=ACT.Abs_reciprocal_sqrt, scale=1.0 / D, bias=eps[:]
+            )
+            rstd_of[r] = rstd
+            result_of[r] = result
+
+        low = slice(0, HALF)
+        high = slice(HALF, D)
+
+        def fold_gains(r):
+            tables = tables_of[r]
+            folded = fold.tile([P, 2, GAINS, TILES_PER_ROUND, D], F32)
+
+            def over_gains(table, columns, width):
+                return tables[:, table, :, columns].unsqueeze(1).to_broadcast([P, GAINS, TILES_PER_ROUND, width])
+
+            def over_tiles(columns, width):
+                return gains[:, :, columns].unsqueeze(2).to_broadcast([P, GAINS, TILES_PER_ROUND, width])
+
+            whole = slice(0, D)
+            nc.gpsimd.tensor_tensor(
+                out=folded[:, COS, :, :, :], in0=over_gains(COS, whole, D), in1=over_tiles(whole, D), op=ALU.mult
+            )
+            nc.gpsimd.tensor_tensor(
+                out=folded[:, SIN, :, :, low], in0=over_gains(SIN, high, HALF), in1=over_tiles(low, HALF), op=ALU.mult
+            )
+            nc.gpsimd.tensor_tensor(
+                out=folded[:, SIN, :, :, high], in0=over_gains(SIN, low, HALF), in1=over_tiles(high, HALF), op=ALU.mult
+            )
+            folded_of[r] = folded
+
+        def scale_by_tables(r):
+            scaled = stage.tile([P, 2, ROTATED, TILES_PER_ROUND, D], F32)
             for t in range(TILES_PER_ROUND):
                 for h in range(ROTATED):
-                    nc.scalar.activation(
-                        out=factors[:, h, t, :], in_=gain_of_head[h][:], func=ACT.Copy, scale=rstd[:, h, t : t + 1]
-                    )
-            factors_of[r] = factors
-            result_of[r] = result
-        def normalise(r):
-            normed = stage.tile([P, ROTATED, TILES_PER_ROUND, D], F32)
-            for t in range(TILES_PER_ROUND):
-                nc.vector.tensor_tensor(
-                    out=normed[:, :, t, :],
-                    in0=product_of[r][t][:, 0 : ROTATED * D].rearrange("p (h d) -> p h d", d=D),
-                    in1=factors_of[r][:, :, t, :],
-                    op=ALU.mult,
-                )
-            normed_of[r] = normed
+                    for table in (COS, SIN):
+                        nc.vector.scalar_tensor_tensor(
+                            out=scaled[:, table, h, t, :],
+                            in0=product_of[r][t][:, h * D : (h + 1) * D],
+                            scalar=rstd_of[r][:, h, t : t + 1],
+                            in1=folded_of[r][:, table, gain_of_head[h], t, :],
+                            op0=ALU.mult,
+                            op1=ALU.mult,
+                        )
+            scaled_of[r] = scaled
 
-        def rotate_and_store(r):
+        def join_and_store(r):
+            scaled = scaled_of[r]
             first = r * TILES_PER_ROUND
             tiles = slice(first, first + TILES_PER_ROUND)
-            low = slice(0, HALF)
-            high = slice(HALF, D)
-            normed = normed_of[r]
             result = result_of[r]
-
-            def over_heads(table, columns, width):
-                return table[:, tiles, columns].unsqueeze(1).to_broadcast([P, ROTATED, TILES_PER_ROUND, width])
-
-            with_cos = stage.tile([P, ROTATED, TILES_PER_ROUND, D], F32)
-            with_sin = stage.tile([P, ROTATED, TILES_PER_ROUND, D], F32)
-            nc.vector.tensor_tensor(out=with_cos[:], in0=normed[:], in1=over_heads(cos_sb, slice(0, D), D), op=ALU.mult)
             nc.vector.tensor_tensor(
-                out=with_sin[:, :, :, low], in0=normed[:, :, :, high], in1=over_heads(sin_sb, low, HALF), op=ALU.mult
+                out=result[:, 0:ROTATED, :, low], in0=scaled[:, COS, :, :, low], in1=scaled[:, SIN, :, :, high], op=ALU.subtract
             )
             nc.vector.tensor_tensor(
-                out=with_sin[:, :, :, high], in0=normed[:, :, :, low], in1=over_heads(sin_sb, high, HALF), op=ALU.mult
-            )
-            nc.vector.tensor_tensor(
-                out=result[:, 0:ROTATED, :, low], in0=with_cos[:, :, :, low], in1=with_sin[:, :, :, low], op=ALU.subtract
-            )
-            nc.vector.tensor_tensor(
-                out=result[:, 0:ROTATED, :, high], in0=with_cos[:, :, :, high], in1=with_sin[:, :, :, high], op=ALU.add
+                out=result[:, 0:ROTATED, :, high], in0=scaled[:, COS, :, :, high], in1=scaled[:, SIN, :, :, low], op=ALU.add
             )
             nc.sync.dma_start(out=q_view[:, :, tiles, :], in_=result[:, 0:2, :, :])
             nc.sync.dma_start(out=k_view[:, tiles, :], in_=result[:, 2, :, :])
@@ -258,9 +268,11 @@ def tile_refattention_pa_t_kernel(
                 regroup(i + 2)
             if in_range(i + 1):
                 norm_factors(i + 1)
+            if in_range(i + 2):
+                fold_gains(i + 2)
             if in_range(i):
-                normalise(i)
+                scale_by_tables(i)
             if in_range(i + 2):
                 quantise(i + 2)
             if in_range(i):
-                rotate_and_store(i)
+                join_and_store(i)

@@ -22,8 +22,9 @@ HALF = D // 2
 EPS = 1e-6
 HEADS = 4
 ROTATED = 3
+Q_HEADS = 2
+K_HEAD = 2
 V_HEAD = 3
-GAINS = 2
 COS = 0
 SIN = 1
 FEATURES = HEADS * D
@@ -44,12 +45,13 @@ def tile_refattention_pa_t_kernel(
 ):
     nc = tc.nc
 
-    x_view = hidden_states.flatten_outer_dims().rearrange("(p j) k -> p j k", j=TILES)
-    cos_view = cos.flatten_outer_dims().rearrange("(p j) d -> p j d", j=TILES)
-    sin_view = sin.flatten_outer_dims().rearrange("(p j) d -> p j d", j=TILES)
-    q_view = out_0.flatten_outer_dims().rearrange("(h p j) d -> p h j d", h=2, j=TILES)
-    k_view = out_1.flatten_outer_dims().rearrange("(p j) d -> p j d", j=TILES)
-    v_view = out_2.flatten_outer_dims().rearrange("(p j) d -> p j d", j=TILES)
+    per_round = TILES_PER_ROUND
+    x_view = hidden_states.flatten_outer_dims().rearrange("(r p t) k -> p r t k", p=P, t=per_round)
+    cos_view = cos.flatten_outer_dims().rearrange("(r p t) d -> p r t d", p=P, t=per_round)
+    sin_view = sin.flatten_outer_dims().rearrange("(r p t) d -> p r t d", p=P, t=per_round)
+    q_view = out_0.flatten_outer_dims().rearrange("(h r p t) d -> p h r t d", h=2, p=P, t=per_round)
+    k_view = out_1.flatten_outer_dims().rearrange("(r p t) d -> p r t d", p=P, t=per_round)
+    v_view = out_2.flatten_outer_dims().rearrange("(r p t) d -> p r t d", p=P, t=per_round)
 
     with ExitStack() as stack:
         stack.enter_context(tc.manual_schedule())
@@ -62,27 +64,24 @@ def tile_refattention_pa_t_kernel(
         psum_turn = stack.enter_context(tc.psum_pool(name="psum_turn", bufs=2 * TILES_PER_ROUND))
         psum_prod = stack.enter_context(tc.psum_pool(name="psum_prod", bufs=2 * TILES_PER_ROUND))
 
-        gains = consts.tile([P, GAINS, D], BF16)
-        nc.scalar.dma_start(out=gains[:, 0, :], in_=q_norm_w.partition_broadcast(P))
-        nc.scalar.dma_start(out=gains[:, 1, :], in_=k_norm_w.partition_broadcast(P))
-        gain_of_head = [0, 0, 1]
+        gain_q = consts.tile([P, D], BF16)
+        gain_k = consts.tile([P, D], BF16)
+        nc.scalar.dma_start(out=gain_q[:], in_=q_norm_w.partition_broadcast(P))
+        nc.scalar.dma_start(out=gain_k[:], in_=k_norm_w.partition_broadcast(P))
 
         w_raw = consts.tile([P, HEADS, HID], BF16)
-        nc.sync.dma_start(out=w_raw[:, 0:2, :], in_=Wq.rearrange("(h p) k -> p h k", p=P))
-        nc.sync.dma_start(out=w_raw[:, 2, :], in_=Wk)
-        nc.sync.dma_start(out=w_raw[:, 3, :], in_=Wv)
+        for h, rows in enumerate((Wq[0:D, :], Wq[D : 2 * D, :], Wk, Wv)):
+            nc.sync.dma_start(out=w_raw[:, h, :], in_=rows)
 
         x_of = {}
         tables_of = {}
 
         def load_tokens(r):
-            first = r * TILES_PER_ROUND
-            tiles = slice(first, first + TILES_PER_ROUND)
             x_sb = x_pool.tile([P, TILES_PER_ROUND, HID], BF16)
-            nc.sync.dma_start(out=x_sb[:], in_=x_view[:, tiles, :])
+            nc.sync.dma_start(out=x_sb[:], in_=x_view[:, r, :, :])
             tables = x_pool.tile([P, 2, TILES_PER_ROUND, D], BF16)
-            nc.sync.dma_start(out=tables[:, COS, :, :], in_=cos_view[:, tiles, :])
-            nc.sync.dma_start(out=tables[:, SIN, :, :], in_=sin_view[:, tiles, :])
+            nc.sync.dma_start(out=tables[:, COS, :, :], in_=cos_view[:, r, :, :])
+            nc.sync.dma_start(out=tables[:, SIN, :, :], in_=sin_view[:, r, :, :])
             x_of[r] = x_sb
             tables_of[r] = tables
 
@@ -128,7 +127,8 @@ def tile_refattention_pa_t_kernel(
         rstd_of = {}
         result_of = {}
         folded_of = {}
-        scaled_of = {}
+        terms_of = {}
+        normed_of = {}
 
         def transpose_tokens(r):
             x_words = x_of[r][:].bitcast(F32)
@@ -156,34 +156,40 @@ def tile_refattention_pa_t_kernel(
             product_of[r] = []
             for t in range(TILES_PER_ROUND):
                 product = psum_prod.tile([P, FEATURES], F32)
-                for repeat in range(2):
-                    for g in range(PASSES):
-                        nc.tensor.matmul_mx(
-                            out=product[:],
-                            lhsT=codes[:, t, g, :].bitcast(FP8X4),
-                            lhsT_scale=scales[:, t, g, :],
-                            rhs=w_codes[:, g, :].bitcast(FP8X4),
-                            rhs_scale=w_scales[:, g, :],
-                            start=(g == 0),
-                            stop=(g == PASSES - 1),
-                        )
+                for g in range(PASSES):
+                    nc.tensor.matmul_mx(
+                        out=product[:],
+                        lhsT=codes[:, t, g, :].bitcast(FP8X4),
+                        lhsT_scale=scales[:, t, g, :],
+                        rhs=w_codes[:, g, :].bitcast(FP8X4),
+                        rhs_scale=w_scales[:, g, :],
+                        start=(g == 0),
+                        stop=(g == PASSES - 1),
+                    )
                 product_of[r].append(product)
 
         def norm_factors(r):
             sum_sq = stats.tile([P, HEADS, TILES_PER_ROUND], F32)
             squares = stage.tile([P, HEADS, TILES_PER_ROUND, D], BF16)
-            for t in range(TILES_PER_ROUND):
-                for h in range(HEADS):
-                    nc.scalar.activation(
-                        out=squares[:, h, t, :],
-                        in_=product_of[r][t][:, h * D : (h + 1) * D],
-                        func=ACT.Square,
-                        accum_out=sum_sq[:, h, t : t + 1],
-                    )
+
+            def sum_squares(t, h):
+                nc.scalar.activation(
+                    out=squares[:, h, t, :],
+                    in_=product_of[r][t][:, h * D : (h + 1) * D],
+                    func=ACT.Square,
+                    accum_out=sum_sq[:, h, t : t + 1],
+                )
+
+            def reciprocal_rms(out, sums):
+                nc.scalar.activation(out=out, in_=sums, func=ACT.Abs_reciprocal_sqrt, scale=1.0 / D, bias=eps[:])
+
+            sums_in_order = [(t, h) for t in range(TILES_PER_ROUND) for h in (V_HEAD, 0, 1, 2)]
+            for t, h in sums_in_order[:-2]:
+                sum_squares(t, h)
             rstd_v = stats.tile([P, TILES_PER_ROUND], F32)
-            nc.scalar.activation(
-                out=rstd_v[:], in_=sum_sq[:, V_HEAD, :], func=ACT.Abs_reciprocal_sqrt, scale=1.0 / D, bias=eps[:]
-            )
+            reciprocal_rms(rstd_v[:], sum_sq[:, V_HEAD, :])
+            for t, h in sums_in_order[-2:]:
+                sum_squares(t, h)
             result = results.tile([P, HEADS, TILES_PER_ROUND, D], F32)
             for t in range(TILES_PER_ROUND):
                 nc.scalar.activation(
@@ -193,66 +199,71 @@ def tile_refattention_pa_t_kernel(
                     scale=rstd_v[:, t : t + 1],
                 )
             rstd = stats.tile([P, ROTATED, TILES_PER_ROUND], F32)
-            nc.scalar.activation(
-                out=rstd[:], in_=sum_sq[:, 0:ROTATED, :], func=ACT.Abs_reciprocal_sqrt, scale=1.0 / D, bias=eps[:]
-            )
+            reciprocal_rms(rstd[:], sum_sq[:, 0:ROTATED, :])
             rstd_of[r] = rstd
             result_of[r] = result
 
         low = slice(0, HALF)
         high = slice(HALF, D)
+        other_half = ((high, low), (low, high))
 
-        def fold_gains(r):
+        def over_tiles(gain, columns, width):
+            return gain[:, columns].unsqueeze(1).to_broadcast([P, TILES_PER_ROUND, width])
+
+        def fold_q_gain(r):
             tables = tables_of[r]
-            folded = fold.tile([P, 2, GAINS, TILES_PER_ROUND, D], F32)
-
-            def over_gains(table, columns, width):
-                return tables[:, table, :, columns].unsqueeze(1).to_broadcast([P, GAINS, TILES_PER_ROUND, width])
-
-            def over_tiles(columns, width):
-                return gains[:, :, columns].unsqueeze(2).to_broadcast([P, GAINS, TILES_PER_ROUND, width])
-
-            whole = slice(0, D)
+            folded = fold.tile([P, 2, TILES_PER_ROUND, D], F32)
             nc.gpsimd.tensor_tensor(
-                out=folded[:, COS, :, :, :], in0=over_gains(COS, whole, D), in1=over_tiles(whole, D), op=ALU.mult
+                out=folded[:, COS, :, :], in0=tables[:, COS, :, :], in1=over_tiles(gain_q, slice(0, D), D), op=ALU.mult
             )
-            nc.gpsimd.tensor_tensor(
-                out=folded[:, SIN, :, :, low], in0=over_gains(SIN, high, HALF), in1=over_tiles(low, HALF), op=ALU.mult
-            )
-            nc.gpsimd.tensor_tensor(
-                out=folded[:, SIN, :, :, high], in0=over_gains(SIN, low, HALF), in1=over_tiles(high, HALF), op=ALU.mult
-            )
+            for here, there in other_half:
+                nc.gpsimd.tensor_tensor(
+                    out=folded[:, SIN, :, here], in0=tables[:, SIN, :, there], in1=over_tiles(gain_q, here, HALF), op=ALU.mult
+                )
             folded_of[r] = folded
 
-        def scale_by_tables(r):
-            scaled = stage.tile([P, 2, ROTATED, TILES_PER_ROUND, D], F32)
-            for t in range(TILES_PER_ROUND):
-                for h in range(ROTATED):
-                    for table in (COS, SIN):
-                        nc.vector.scalar_tensor_tensor(
-                            out=scaled[:, table, h, t, :],
-                            in0=product_of[r][t][:, h * D : (h + 1) * D],
-                            scalar=rstd_of[r][:, h, t : t + 1],
-                            in1=folded_of[r][:, table, gain_of_head[h], t, :],
-                            op0=ALU.mult,
-                            op1=ALU.mult,
-                        )
-            scaled_of[r] = scaled
+        def scale_products(r):
+            normed_k = stage.tile([P, TILES_PER_ROUND, D], F32)
+            terms = stage.tile([P, 2, ROTATED, TILES_PER_ROUND, D], F32)
 
-        def join_and_store(r):
-            scaled = scaled_of[r]
-            first = r * TILES_PER_ROUND
-            tiles = slice(first, first + TILES_PER_ROUND)
+            def times_rstd_times(out, t, h, in1):
+                nc.vector.scalar_tensor_tensor(
+                    out=out,
+                    in0=product_of[r][t][:, h * D : (h + 1) * D],
+                    scalar=rstd_of[r][:, h, t : t + 1],
+                    in1=in1,
+                    op0=ALU.mult,
+                    op1=ALU.mult,
+                )
+
+            for t in range(TILES_PER_ROUND):
+                times_rstd_times(normed_k[:, t, :], t, K_HEAD, gain_k[:])
+            for t in range(TILES_PER_ROUND):
+                for h in range(Q_HEADS):
+                    for table in (COS, SIN):
+                        times_rstd_times(terms[:, table, h, t, :], t, h, folded_of[r][:, table, t, :])
+            normed_of[r] = normed_k
+            terms_of[r] = terms
+
+        def rotate_and_store(r):
+            tables = tables_of[r]
+            normed_k = normed_of[r]
+            terms = terms_of[r]
             result = result_of[r]
+            nc.vector.tensor_tensor(out=terms[:, COS, K_HEAD, :, :], in0=normed_k[:], in1=tables[:, COS, :, :], op=ALU.mult)
+            for here, there in other_half:
+                nc.vector.tensor_tensor(
+                    out=terms[:, SIN, K_HEAD, :, here], in0=normed_k[:, :, here], in1=tables[:, SIN, :, there], op=ALU.mult
+                )
             nc.vector.tensor_tensor(
-                out=result[:, 0:ROTATED, :, low], in0=scaled[:, COS, :, :, low], in1=scaled[:, SIN, :, :, high], op=ALU.subtract
+                out=result[:, 0:ROTATED, :, low], in0=terms[:, COS, :, :, low], in1=terms[:, SIN, :, :, high], op=ALU.subtract
             )
             nc.vector.tensor_tensor(
-                out=result[:, 0:ROTATED, :, high], in0=scaled[:, COS, :, :, high], in1=scaled[:, SIN, :, :, low], op=ALU.add
+                out=result[:, 0:ROTATED, :, high], in0=terms[:, COS, :, :, high], in1=terms[:, SIN, :, :, low], op=ALU.add
             )
-            nc.sync.dma_start(out=q_view[:, :, tiles, :], in_=result[:, 0:2, :, :])
-            nc.sync.dma_start(out=k_view[:, tiles, :], in_=result[:, 2, :, :])
-            nc.sync.dma_start(out=v_view[:, tiles, :], in_=result[:, V_HEAD, :, :])
+            nc.sync.dma_start(out=q_view[:, :, r, :, :], in_=result[:, 0:Q_HEADS, :, :])
+            nc.sync.dma_start(out=k_view[:, r, :, :], in_=result[:, K_HEAD, :, :])
+            nc.sync.dma_start(out=v_view[:, r, :, :], in_=result[:, V_HEAD, :, :])
 
         def in_range(r):
             return 0 <= r < ROUNDS
@@ -269,10 +280,10 @@ def tile_refattention_pa_t_kernel(
             if in_range(i + 1):
                 norm_factors(i + 1)
             if in_range(i + 2):
-                fold_gains(i + 2)
+                fold_q_gain(i + 2)
             if in_range(i):
-                scale_by_tables(i)
+                scale_products(i)
             if in_range(i + 2):
                 quantise(i + 2)
             if in_range(i):
-                join_and_store(i)
+                rotate_and_store(i)

@@ -22,11 +22,7 @@ HALF = D // 2
 EPS = 1e-6
 HEADS = 4
 ROTATED = 3
-Q_HEADS = 2
-K_HEAD = 2
 V_HEAD = 3
-COS = 0
-SIN = 1
 FEATURES = HEADS * D
 
 PASSES = HID // K_PASS
@@ -45,13 +41,12 @@ def tile_refattention_pa_t_kernel(
 ):
     nc = tc.nc
 
-    per_round = TILES_PER_ROUND
-    x_view = hidden_states.flatten_outer_dims().rearrange("(r p t) k -> p r t k", p=P, t=per_round)
-    cos_view = cos.flatten_outer_dims().rearrange("(r p t) d -> p r t d", p=P, t=per_round)
-    sin_view = sin.flatten_outer_dims().rearrange("(r p t) d -> p r t d", p=P, t=per_round)
-    q_view = out_0.flatten_outer_dims().rearrange("(h r p t) d -> p h r t d", h=2, p=P, t=per_round)
-    k_view = out_1.flatten_outer_dims().rearrange("(r p t) d -> p r t d", p=P, t=per_round)
-    v_view = out_2.flatten_outer_dims().rearrange("(r p t) d -> p r t d", p=P, t=per_round)
+    x_view = hidden_states.flatten_outer_dims().rearrange("(p j) k -> p j k", j=TILES)
+    cos_view = cos.flatten_outer_dims().rearrange("(p j) d -> p j d", j=TILES)
+    sin_view = sin.flatten_outer_dims().rearrange("(p j) d -> p j d", j=TILES)
+    q_view = out_0.flatten_outer_dims().rearrange("(h p j) d -> p h j d", h=2, j=TILES)
+    k_view = out_1.flatten_outer_dims().rearrange("(p j) d -> p j d", j=TILES)
+    v_view = out_2.flatten_outer_dims().rearrange("(p j) d -> p j d", j=TILES)
 
     with ExitStack() as stack:
         stack.enter_context(tc.manual_schedule())
@@ -59,39 +54,40 @@ def tile_refattention_pa_t_kernel(
         x_pool = stack.enter_context(tc.tile_pool(name="x", bufs=ROUNDS))
         stage = stack.enter_context(tc.tile_pool(name="stage", bufs=2))
         stats = stack.enter_context(tc.tile_pool(name="stats", bufs=3))
-        fold = stack.enter_context(tc.tile_pool(name="fold", bufs=3))
+        ring = stack.enter_context(tc.tile_pool(name="ring", bufs=3))
         results = stack.enter_context(tc.tile_pool(name="results", bufs=4))
         psum_turn = stack.enter_context(tc.psum_pool(name="psum_turn", bufs=2 * TILES_PER_ROUND))
         psum_prod = stack.enter_context(tc.psum_pool(name="psum_prod", bufs=2 * TILES_PER_ROUND))
 
-        gain_q = consts.tile([P, D], BF16)
-        gain_k = consts.tile([P, D], BF16)
-        nc.scalar.dma_start(out=gain_q[:], in_=q_norm_w.partition_broadcast(P))
-        nc.scalar.dma_start(out=gain_k[:], in_=k_norm_w.partition_broadcast(P))
+        gains = consts.tile([P, ROTATED, D], BF16)
+        nc.scalar.dma_start(out=gains[:, 0, :], in_=q_norm_w.partition_broadcast(P))
+        nc.scalar.dma_start(out=gains[:, 2, :], in_=k_norm_w.partition_broadcast(P))
 
         w_raw = consts.tile([P, HEADS, HID], BF16)
         for h, rows in enumerate((Wq[0:D, :], Wq[D : 2 * D, :], Wk, Wv)):
             nc.sync.dma_start(out=w_raw[:, h, :], in_=rows)
 
         x_of = {}
-        tables_of = {}
 
         def load_tokens(r):
             x_sb = x_pool.tile([P, TILES_PER_ROUND, HID], BF16)
-            nc.sync.dma_start(out=x_sb[:], in_=x_view[:, r, :, :])
-            tables = x_pool.tile([P, 2, TILES_PER_ROUND, D], BF16)
-            nc.sync.dma_start(out=tables[:, COS, :, :], in_=cos_view[:, r, :, :])
-            nc.sync.dma_start(out=tables[:, SIN, :, :], in_=sin_view[:, r, :, :])
+            first = r * TILES_PER_ROUND
+            nc.sync.dma_start(out=x_sb[:], in_=x_view[:, first : first + TILES_PER_ROUND, :])
             x_of[r] = x_sb
-            tables_of[r] = tables
 
-        for r in range(LOAD_AHEAD - 3):
-            load_tokens(r)
+        cos_sb = consts.tile([P, TILES, D], BF16)
+        sin_sb = consts.tile([P, TILES, D], BF16)
+        load_tokens(0)
+        load_tokens(1)
+        nc.sync.dma_start(out=cos_sb[:], in_=cos_view)
+        nc.sync.dma_start(out=sin_sb[:], in_=sin_view)
+        load_tokens(2)
 
         identity = consts.tile([P, P], F32)
         make_identity(nc, identity[:])
         eps = consts.tile([P, 1], F32)
         nc.vector.memset(eps[:], EPS)
+        nc.vector.tensor_copy(out=gains[:, 1, :], in_=gains[:, 0, :])
         table_warmer = consts.tile([P, 1], F32)
         nc.scalar.activation(out=table_warmer[:], in_=eps[:], func=ACT.Abs_reciprocal_sqrt)
 
@@ -124,10 +120,8 @@ def tile_refattention_pa_t_kernel(
         grouped_of = {}
         codes_of = {}
         product_of = {}
-        rstd_of = {}
+        gained_of = {}
         result_of = {}
-        folded_of = {}
-        terms_of = {}
         normed_of = {}
 
         def transpose_tokens(r):
@@ -168,102 +162,87 @@ def tile_refattention_pa_t_kernel(
                     )
                 product_of[r].append(product)
 
-        def norm_factors(r):
-            sum_sq = stats.tile([P, HEADS, TILES_PER_ROUND], F32)
-            squares = stage.tile([P, HEADS, TILES_PER_ROUND, D], BF16)
+        def normalise(r):
+            sum_sq = stats.tile([P, TILES_PER_ROUND, HEADS], F32)
+            rstd = stats.tile([P, TILES_PER_ROUND, HEADS], F32)
+            squares = stage.tile([P, TILES_PER_ROUND, HEADS, D], BF16)
+            normed = ring.tile([P, ROTATED, TILES_PER_ROUND, D], F32)
+            result = results.tile([P, HEADS, TILES_PER_ROUND, D], F32)
 
             def sum_squares(t, h):
                 nc.scalar.activation(
-                    out=squares[:, h, t, :],
+                    out=squares[:, t, h, :],
                     in_=product_of[r][t][:, h * D : (h + 1) * D],
                     func=ACT.Square,
-                    accum_out=sum_sq[:, h, t : t + 1],
+                    accum_out=sum_sq[:, t, h : h + 1],
                 )
 
-            def reciprocal_rms(out, sums):
-                nc.scalar.activation(out=out, in_=sums, func=ACT.Abs_reciprocal_sqrt, scale=1.0 / D, bias=eps[:])
-
-            sums_in_order = [(t, h) for t in range(TILES_PER_ROUND) for h in (V_HEAD, 0, 1, 2)]
-            for t, h in sums_in_order[:-2]:
-                sum_squares(t, h)
-            rstd_v = stats.tile([P, TILES_PER_ROUND], F32)
-            reciprocal_rms(rstd_v[:], sum_sq[:, V_HEAD, :])
-            for t, h in sums_in_order[-2:]:
-                sum_squares(t, h)
-            result = results.tile([P, HEADS, TILES_PER_ROUND, D], F32)
-            for t in range(TILES_PER_ROUND):
+            def reciprocal_rms(t):
                 nc.scalar.activation(
-                    out=result[:, V_HEAD, t, :],
-                    in_=product_of[r][t][:, V_HEAD * D : FEATURES],
-                    func=ACT.Copy,
-                    scale=rstd_v[:, t : t + 1],
+                    out=rstd[:, t, :], in_=sum_sq[:, t, :], func=ACT.Abs_reciprocal_sqrt, scale=1.0 / D, bias=eps[:]
                 )
-            rstd = stats.tile([P, ROTATED, TILES_PER_ROUND], F32)
-            reciprocal_rms(rstd[:], sum_sq[:, 0:ROTATED, :])
-            rstd_of[r] = rstd
+
+            def times_rstd(t, h):
+                nc.scalar.activation(
+                    out=result[:, V_HEAD, t, :] if h == V_HEAD else normed[:, h, t, :],
+                    in_=product_of[r][t][:, h * D : (h + 1) * D],
+                    func=ACT.Copy,
+                    scale=rstd[:, t, h : h + 1],
+                )
+
+            every = [(t, h) for t in range(TILES_PER_ROUND) for h in range(HEADS)]
+            for t, h in every[:-2]:
+                sum_squares(t, h)
+            reciprocal_rms(0)
+            for t, h in every[-2:]:
+                sum_squares(t, h)
+            for t, h in every[: HEADS - 1]:
+                times_rstd(t, h)
+            reciprocal_rms(1)
+            for t, h in every[HEADS - 1 :]:
+                times_rstd(t, h)
+            normed_of[r] = normed
             result_of[r] = result
 
-        low = slice(0, HALF)
-        high = slice(HALF, D)
-        other_half = ((high, low), (low, high))
-
-        def over_tiles(gain, columns, width):
-            return gain[:, columns].unsqueeze(1).to_broadcast([P, TILES_PER_ROUND, width])
-
-        def fold_q_gain(r):
-            tables = tables_of[r]
-            folded = fold.tile([P, 2, TILES_PER_ROUND, D], F32)
-            nc.gpsimd.tensor_tensor(
-                out=folded[:, COS, :, :], in0=tables[:, COS, :, :], in1=over_tiles(gain_q, slice(0, D), D), op=ALU.mult
+        def apply_gains(r):
+            gained = stage.tile([P, ROTATED, TILES_PER_ROUND, D], F32)
+            nc.vector.tensor_tensor(
+                out=gained[:],
+                in0=normed_of[r][:],
+                in1=gains[:].unsqueeze(2).to_broadcast([P, ROTATED, TILES_PER_ROUND, D]),
+                op=ALU.mult,
             )
-            for here, there in other_half:
-                nc.gpsimd.tensor_tensor(
-                    out=folded[:, SIN, :, here], in0=tables[:, SIN, :, there], in1=over_tiles(gain_q, here, HALF), op=ALU.mult
-                )
-            folded_of[r] = folded
-
-        def scale_products(r):
-            normed_k = stage.tile([P, TILES_PER_ROUND, D], F32)
-            terms = stage.tile([P, 2, ROTATED, TILES_PER_ROUND, D], F32)
-
-            def times_rstd_times(out, t, h, in1):
-                nc.vector.scalar_tensor_tensor(
-                    out=out,
-                    in0=product_of[r][t][:, h * D : (h + 1) * D],
-                    scalar=rstd_of[r][:, h, t : t + 1],
-                    in1=in1,
-                    op0=ALU.mult,
-                    op1=ALU.mult,
-                )
-
-            for t in range(TILES_PER_ROUND):
-                times_rstd_times(normed_k[:, t, :], t, K_HEAD, gain_k[:])
-            for t in range(TILES_PER_ROUND):
-                for h in range(Q_HEADS):
-                    for table in (COS, SIN):
-                        times_rstd_times(terms[:, table, h, t, :], t, h, folded_of[r][:, table, t, :])
-            normed_of[r] = normed_k
-            terms_of[r] = terms
+            gained_of[r] = gained
 
         def rotate_and_store(r):
-            tables = tables_of[r]
-            normed_k = normed_of[r]
-            terms = terms_of[r]
+            first = r * TILES_PER_ROUND
+            tiles = slice(first, first + TILES_PER_ROUND)
+            low = slice(0, HALF)
+            high = slice(HALF, D)
             result = result_of[r]
-            nc.vector.tensor_tensor(out=terms[:, COS, K_HEAD, :, :], in0=normed_k[:], in1=tables[:, COS, :, :], op=ALU.mult)
-            for here, there in other_half:
-                nc.vector.tensor_tensor(
-                    out=terms[:, SIN, K_HEAD, :, here], in0=normed_k[:, :, here], in1=tables[:, SIN, :, there], op=ALU.mult
-                )
+
+            def over_heads(table, columns, width):
+                return table[:, tiles, columns].unsqueeze(1).to_broadcast([P, ROTATED, TILES_PER_ROUND, width])
+
+            gained = gained_of[r]
+            with_cos = stage.tile([P, ROTATED, TILES_PER_ROUND, D], F32)
+            with_sin = stage.tile([P, ROTATED, TILES_PER_ROUND, D], F32)
+            nc.vector.tensor_tensor(out=with_cos[:], in0=gained[:], in1=over_heads(cos_sb, slice(0, D), D), op=ALU.mult)
             nc.vector.tensor_tensor(
-                out=result[:, 0:ROTATED, :, low], in0=terms[:, COS, :, :, low], in1=terms[:, SIN, :, :, high], op=ALU.subtract
+                out=with_sin[:, :, :, low], in0=gained[:, :, :, high], in1=over_heads(sin_sb, low, HALF), op=ALU.mult
             )
             nc.vector.tensor_tensor(
-                out=result[:, 0:ROTATED, :, high], in0=terms[:, COS, :, :, high], in1=terms[:, SIN, :, :, low], op=ALU.add
+                out=with_sin[:, :, :, high], in0=gained[:, :, :, low], in1=over_heads(sin_sb, high, HALF), op=ALU.mult
             )
-            nc.sync.dma_start(out=q_view[:, :, r, :, :], in_=result[:, 0:Q_HEADS, :, :])
-            nc.sync.dma_start(out=k_view[:, r, :, :], in_=result[:, K_HEAD, :, :])
-            nc.sync.dma_start(out=v_view[:, r, :, :], in_=result[:, V_HEAD, :, :])
+            nc.vector.tensor_tensor(
+                out=result[:, 0:ROTATED, :, low], in0=with_cos[:, :, :, low], in1=with_sin[:, :, :, low], op=ALU.subtract
+            )
+            nc.vector.tensor_tensor(
+                out=result[:, 0:ROTATED, :, high], in0=with_cos[:, :, :, high], in1=with_sin[:, :, :, high], op=ALU.add
+            )
+            nc.sync.dma_start(out=q_view[:, :, tiles, :], in_=result[:, 0:2, :, :])
+            nc.sync.dma_start(out=k_view[:, tiles, :], in_=result[:, 2, :, :])
+            nc.sync.dma_start(out=v_view[:, tiles, :], in_=result[:, V_HEAD, :, :])
 
         def in_range(r):
             return 0 <= r < ROUNDS
@@ -278,11 +257,9 @@ def tile_refattention_pa_t_kernel(
             if in_range(i + 2):
                 regroup(i + 2)
             if in_range(i + 1):
-                norm_factors(i + 1)
-            if in_range(i + 2):
-                fold_q_gain(i + 2)
+                normalise(i + 1)
             if in_range(i):
-                scale_products(i)
+                apply_gains(i)
             if in_range(i + 2):
                 quantise(i + 2)
             if in_range(i):

@@ -22,7 +22,11 @@ HALF = D // 2
 EPS = 1e-6
 HEADS = 4
 ROTATED = 3
+Q_HEADS = 2
+K_HEAD = 2
 V_HEAD = 3
+COS = 0
+SIN = 1
 FEATURES = HEADS * D
 
 PASSES = HID // K_PASS
@@ -54,40 +58,41 @@ def tile_refattention_pa_t_kernel(
         x_pool = stack.enter_context(tc.tile_pool(name="x", bufs=ROUNDS))
         stage = stack.enter_context(tc.tile_pool(name="stage", bufs=2))
         stats = stack.enter_context(tc.tile_pool(name="stats", bufs=3))
-        ring = stack.enter_context(tc.tile_pool(name="ring", bufs=3))
+        fold = stack.enter_context(tc.tile_pool(name="fold", bufs=3))
         results = stack.enter_context(tc.tile_pool(name="results", bufs=4))
         psum_turn = stack.enter_context(tc.psum_pool(name="psum_turn", bufs=2 * TILES_PER_ROUND))
         psum_prod = stack.enter_context(tc.psum_pool(name="psum_prod", bufs=2 * TILES_PER_ROUND))
 
-        gains = consts.tile([P, ROTATED, D], BF16)
-        nc.scalar.dma_start(out=gains[:, 0, :], in_=q_norm_w.partition_broadcast(P))
-        nc.scalar.dma_start(out=gains[:, 2, :], in_=k_norm_w.partition_broadcast(P))
+        gain_q = consts.tile([P, D], BF16)
+        gain_k = consts.tile([P, D], BF16)
+        nc.scalar.dma_start(out=gain_q[:], in_=q_norm_w.partition_broadcast(P))
+        nc.scalar.dma_start(out=gain_k[:], in_=k_norm_w.partition_broadcast(P))
 
         w_raw = consts.tile([P, HEADS, HID], BF16)
         for h, rows in enumerate((Wq[0:D, :], Wq[D : 2 * D, :], Wk, Wv)):
             nc.sync.dma_start(out=w_raw[:, h, :], in_=rows)
 
         x_of = {}
+        tables_of = {}
 
         def load_tokens(r):
-            x_sb = x_pool.tile([P, TILES_PER_ROUND, HID], BF16)
             first = r * TILES_PER_ROUND
-            nc.sync.dma_start(out=x_sb[:], in_=x_view[:, first : first + TILES_PER_ROUND, :])
+            tiles = slice(first, first + TILES_PER_ROUND)
+            x_sb = x_pool.tile([P, TILES_PER_ROUND, HID], BF16)
+            nc.sync.dma_start(out=x_sb[:], in_=x_view[:, tiles, :])
+            tables = x_pool.tile([P, 2, TILES_PER_ROUND, D], BF16)
+            nc.sync.dma_start(out=tables[:, COS, :, :], in_=cos_view[:, tiles, :])
+            nc.sync.dma_start(out=tables[:, SIN, :, :], in_=sin_view[:, tiles, :])
             x_of[r] = x_sb
+            tables_of[r] = tables
 
-        cos_sb = consts.tile([P, TILES, D], BF16)
-        sin_sb = consts.tile([P, TILES, D], BF16)
-        load_tokens(0)
-        load_tokens(1)
-        nc.sync.dma_start(out=cos_sb[:], in_=cos_view)
-        nc.sync.dma_start(out=sin_sb[:], in_=sin_view)
-        load_tokens(2)
+        for r in range(LOAD_AHEAD - 3):
+            load_tokens(r)
 
         identity = consts.tile([P, P], F32)
         make_identity(nc, identity[:])
         eps = consts.tile([P, 1], F32)
         nc.vector.memset(eps[:], EPS)
-        nc.vector.tensor_copy(out=gains[:, 1, :], in_=gains[:, 0, :])
         table_warmer = consts.tile([P, 1], F32)
         nc.scalar.activation(out=table_warmer[:], in_=eps[:], func=ACT.Abs_reciprocal_sqrt)
 
@@ -120,8 +125,10 @@ def tile_refattention_pa_t_kernel(
         grouped_of = {}
         codes_of = {}
         product_of = {}
-        gained_of = {}
+        rstd_of = {}
         result_of = {}
+        folded_of = {}
+        terms_of = {}
         normed_of = {}
 
         def transpose_tokens(r):
@@ -150,98 +157,116 @@ def tile_refattention_pa_t_kernel(
             product_of[r] = []
             for t in range(TILES_PER_ROUND):
                 product = psum_prod.tile([P, FEATURES], F32)
-                for g in range(PASSES):
-                    nc.tensor.matmul_mx(
-                        out=product[:],
-                        lhsT=codes[:, t, g, :].bitcast(FP8X4),
-                        lhsT_scale=scales[:, t, g, :],
-                        rhs=w_codes[:, g, :].bitcast(FP8X4),
-                        rhs_scale=w_scales[:, g, :],
-                        start=(g == 0),
-                        stop=(g == PASSES - 1),
-                    )
+                for repeat in range(2):
+                    for g in range(PASSES):
+                        nc.tensor.matmul_mx(
+                            out=product[:],
+                            lhsT=codes[:, t, g, :].bitcast(FP8X4),
+                            lhsT_scale=scales[:, t, g, :],
+                            rhs=w_codes[:, g, :].bitcast(FP8X4),
+                            rhs_scale=w_scales[:, g, :],
+                            start=(g == 0),
+                            stop=(g == PASSES - 1),
+                        )
                 product_of[r].append(product)
 
-        def normalise(r):
-            sum_sq = stats.tile([P, TILES_PER_ROUND, HEADS], F32)
-            rstd = stats.tile([P, TILES_PER_ROUND, HEADS], F32)
-            squares = stage.tile([P, TILES_PER_ROUND, HEADS, D], BF16)
-            normed = ring.tile([P, ROTATED, TILES_PER_ROUND, D], F32)
-            result = results.tile([P, HEADS, TILES_PER_ROUND, D], F32)
+        def norm_factors(r):
+            sum_sq = stats.tile([P, HEADS, TILES_PER_ROUND], F32)
+            squares = stage.tile([P, HEADS, TILES_PER_ROUND, D], BF16)
 
             def sum_squares(t, h):
                 nc.scalar.activation(
-                    out=squares[:, t, h, :],
+                    out=squares[:, h, t, :],
                     in_=product_of[r][t][:, h * D : (h + 1) * D],
                     func=ACT.Square,
-                    accum_out=sum_sq[:, t, h : h + 1],
+                    accum_out=sum_sq[:, h, t : t + 1],
                 )
 
-            def reciprocal_rms(t):
-                nc.scalar.activation(
-                    out=rstd[:, t, :], in_=sum_sq[:, t, :], func=ACT.Abs_reciprocal_sqrt, scale=1.0 / D, bias=eps[:]
-                )
+            def reciprocal_rms(out, sums):
+                nc.scalar.activation(out=out, in_=sums, func=ACT.Abs_reciprocal_sqrt, scale=1.0 / D, bias=eps[:])
 
-            def times_rstd(t, h):
+            sums_in_order = [(t, h) for t in range(TILES_PER_ROUND) for h in (V_HEAD, 0, 1, 2)]
+            for t, h in sums_in_order[:-2]:
+                sum_squares(t, h)
+            rstd_v = stats.tile([P, TILES_PER_ROUND], F32)
+            reciprocal_rms(rstd_v[:], sum_sq[:, V_HEAD, :])
+            for t, h in sums_in_order[-2:]:
+                sum_squares(t, h)
+            result = results.tile([P, HEADS, TILES_PER_ROUND, D], F32)
+            for t in range(TILES_PER_ROUND):
                 nc.scalar.activation(
-                    out=result[:, V_HEAD, t, :] if h == V_HEAD else normed[:, h, t, :],
-                    in_=product_of[r][t][:, h * D : (h + 1) * D],
+                    out=result[:, V_HEAD, t, :],
+                    in_=product_of[r][t][:, V_HEAD * D : FEATURES],
                     func=ACT.Copy,
-                    scale=rstd[:, t, h : h + 1],
+                    scale=rstd_v[:, t : t + 1],
                 )
-
-            every = [(t, h) for t in range(TILES_PER_ROUND) for h in range(HEADS)]
-            for t, h in every[:-2]:
-                sum_squares(t, h)
-            reciprocal_rms(0)
-            for t, h in every[-2:]:
-                sum_squares(t, h)
-            for t, h in every[: HEADS - 1]:
-                times_rstd(t, h)
-            reciprocal_rms(1)
-            for t, h in every[HEADS - 1 :]:
-                times_rstd(t, h)
-            normed_of[r] = normed
+            rstd = stats.tile([P, ROTATED, TILES_PER_ROUND], F32)
+            reciprocal_rms(rstd[:], sum_sq[:, 0:ROTATED, :])
+            rstd_of[r] = rstd
             result_of[r] = result
 
-        def apply_gains(r):
-            gained = stage.tile([P, ROTATED, TILES_PER_ROUND, D], F32)
-            nc.vector.tensor_tensor(
-                out=gained[:],
-                in0=normed_of[r][:],
-                in1=gains[:].unsqueeze(2).to_broadcast([P, ROTATED, TILES_PER_ROUND, D]),
-                op=ALU.mult,
+        low = slice(0, HALF)
+        high = slice(HALF, D)
+        other_half = ((high, low), (low, high))
+
+        def over_tiles(gain, columns, width):
+            return gain[:, columns].unsqueeze(1).to_broadcast([P, TILES_PER_ROUND, width])
+
+        def fold_q_gain(r):
+            tables = tables_of[r]
+            folded = fold.tile([P, 2, TILES_PER_ROUND, D], F32)
+            nc.gpsimd.tensor_tensor(
+                out=folded[:, COS, :, :], in0=tables[:, COS, :, :], in1=over_tiles(gain_q, slice(0, D), D), op=ALU.mult
             )
-            gained_of[r] = gained
+            for here, there in other_half:
+                nc.gpsimd.tensor_tensor(
+                    out=folded[:, SIN, :, here], in0=tables[:, SIN, :, there], in1=over_tiles(gain_q, here, HALF), op=ALU.mult
+                )
+            folded_of[r] = folded
+
+        def scale_products(r):
+            normed_k = stage.tile([P, TILES_PER_ROUND, D], F32)
+            terms = stage.tile([P, 2, ROTATED, TILES_PER_ROUND, D], F32)
+
+            def times_rstd_times(out, t, h, in1):
+                nc.vector.scalar_tensor_tensor(
+                    out=out,
+                    in0=product_of[r][t][:, h * D : (h + 1) * D],
+                    scalar=rstd_of[r][:, h, t : t + 1],
+                    in1=in1,
+                    op0=ALU.mult,
+                    op1=ALU.mult,
+                )
+
+            for t in range(TILES_PER_ROUND):
+                times_rstd_times(normed_k[:, t, :], t, K_HEAD, gain_k[:])
+            for t in range(TILES_PER_ROUND):
+                for h in range(Q_HEADS):
+                    for table in (COS, SIN):
+                        times_rstd_times(terms[:, table, h, t, :], t, h, folded_of[r][:, table, t, :])
+            normed_of[r] = normed_k
+            terms_of[r] = terms
 
         def rotate_and_store(r):
             first = r * TILES_PER_ROUND
             tiles = slice(first, first + TILES_PER_ROUND)
-            low = slice(0, HALF)
-            high = slice(HALF, D)
+            tables = tables_of[r]
+            normed_k = normed_of[r]
+            terms = terms_of[r]
             result = result_of[r]
-
-            def over_heads(table, columns, width):
-                return table[:, tiles, columns].unsqueeze(1).to_broadcast([P, ROTATED, TILES_PER_ROUND, width])
-
-            gained = gained_of[r]
-            with_cos = stage.tile([P, ROTATED, TILES_PER_ROUND, D], F32)
-            with_sin = stage.tile([P, ROTATED, TILES_PER_ROUND, D], F32)
-            nc.vector.tensor_tensor(out=with_cos[:], in0=gained[:], in1=over_heads(cos_sb, slice(0, D), D), op=ALU.mult)
+            nc.vector.tensor_tensor(out=terms[:, COS, K_HEAD, :, :], in0=normed_k[:], in1=tables[:, COS, :, :], op=ALU.mult)
+            for here, there in other_half:
+                nc.vector.tensor_tensor(
+                    out=terms[:, SIN, K_HEAD, :, here], in0=normed_k[:, :, here], in1=tables[:, SIN, :, there], op=ALU.mult
+                )
             nc.vector.tensor_tensor(
-                out=with_sin[:, :, :, low], in0=gained[:, :, :, high], in1=over_heads(sin_sb, low, HALF), op=ALU.mult
+                out=result[:, 0:ROTATED, :, low], in0=terms[:, COS, :, :, low], in1=terms[:, SIN, :, :, high], op=ALU.subtract
             )
             nc.vector.tensor_tensor(
-                out=with_sin[:, :, :, high], in0=gained[:, :, :, low], in1=over_heads(sin_sb, high, HALF), op=ALU.mult
+                out=result[:, 0:ROTATED, :, high], in0=terms[:, COS, :, :, high], in1=terms[:, SIN, :, :, low], op=ALU.add
             )
-            nc.vector.tensor_tensor(
-                out=result[:, 0:ROTATED, :, low], in0=with_cos[:, :, :, low], in1=with_sin[:, :, :, low], op=ALU.subtract
-            )
-            nc.vector.tensor_tensor(
-                out=result[:, 0:ROTATED, :, high], in0=with_cos[:, :, :, high], in1=with_sin[:, :, :, high], op=ALU.add
-            )
-            nc.sync.dma_start(out=q_view[:, :, tiles, :], in_=result[:, 0:2, :, :])
-            nc.sync.dma_start(out=k_view[:, tiles, :], in_=result[:, 2, :, :])
+            nc.sync.dma_start(out=q_view[:, :, tiles, :], in_=result[:, 0:Q_HEADS, :, :])
+            nc.sync.dma_start(out=k_view[:, tiles, :], in_=result[:, K_HEAD, :, :])
             nc.sync.dma_start(out=v_view[:, tiles, :], in_=result[:, V_HEAD, :, :])
 
         def in_range(r):
@@ -257,9 +282,11 @@ def tile_refattention_pa_t_kernel(
             if in_range(i + 2):
                 regroup(i + 2)
             if in_range(i + 1):
-                normalise(i + 1)
+                norm_factors(i + 1)
+            if in_range(i + 2):
+                fold_q_gain(i + 2)
             if in_range(i):
-                apply_gains(i)
+                scale_products(i)
             if in_range(i + 2):
                 quantise(i + 2)
             if in_range(i):

from contextlib import ExitStack

import concourse.mybir as mybir
from concourse.masks import make_identity

BF16 = mybir.dt.bfloat16
F32 = mybir.dt.float32
U32 = mybir.dt.uint32
U8 = mybir.dt.uint8
FP8X4 = mybir.dt.float8_e4m3fn_x4
ACT = mybir.ActivationFunctionType
ALU = mybir.AluOpType

P = 128
PACK = 4
K_PASS = P * PACK

TOKENS = 4096
HID = 1024
D = 128
HALF = D // 2
EPS = 1e-6
HEADS = 4
ROTATED = 3
Q_HEADS = 2
K_HEAD = 2
V_HEAD = 3
COS = 0
SIN = 1
FEATURES = HEADS * D

PASSES = HID // K_PASS
WORDS = HID // 2
TURNS = WORDS // P
TILES = TOKENS // P
TILES_PER_ROUND = 2
ROUNDS = TILES // TILES_PER_ROUND
LOAD_AHEAD = 6

FLOPS = 2 * TOKENS * HID * FEATURES


def tile_refattention_pa_t_kernel(
    tc, hidden_states, cos, sin, Wq, Wk, Wv, q_norm_w, k_norm_w, out_0, out_1, out_2
):
    nc = tc.nc

    x_view = hidden_states.flatten_outer_dims().rearrange("(p j) k -> p j k", j=TILES)
    cos_view = cos.flatten_outer_dims().rearrange("(p j) d -> p j d", j=TILES)
    sin_view = sin.flatten_outer_dims().rearrange("(p j) d -> p j d", j=TILES)
    q_view = out_0.flatten_outer_dims().rearrange("(h p j) d -> p h j d", h=2, j=TILES)
    k_view = out_1.flatten_outer_dims().rearrange("(p j) d -> p j d", j=TILES)
    v_view = out_2.flatten_outer_dims().rearrange("(p j) d -> p j d", j=TILES)

    with ExitStack() as stack:
        stack.enter_context(tc.manual_schedule())
        consts = stack.enter_context(tc.tile_pool(name="consts", bufs=1))
        x_pool = stack.enter_context(tc.tile_pool(name="x", bufs=ROUNDS))
        stage = stack.enter_context(tc.tile_pool(name="stage", bufs=2))
        stats = stack.enter_context(tc.tile_pool(name="stats", bufs=3))
        fold = stack.enter_context(tc.tile_pool(name="fold", bufs=3))
        results = stack.enter_context(tc.tile_pool(name="results", bufs=4))
        psum_turn = stack.enter_context(tc.psum_pool(name="psum_turn", bufs=2 * TILES_PER_ROUND))
        psum_prod = stack.enter_context(tc.psum_pool(name="psum_prod", bufs=2 * TILES_PER_ROUND))

        gain_q = consts.tile([P, D], BF16)
        gain_k = consts.tile([P, D], BF16)
        nc.scalar.dma_start(out=gain_q[:], in_=q_norm_w.partition_broadcast(P))
        nc.scalar.dma_start(out=gain_k[:], in_=k_norm_w.partition_broadcast(P))

        w_raw = consts.tile([P, HEADS, HID], BF16)
        for h, rows in enumerate((Wq[0:D, :], Wq[D : 2 * D, :], Wk, Wv)):
            nc.sync.dma_start(out=w_raw[:, h, :], in_=rows)

        x_of = {}
        tables_of = {}

        def load_tokens(r):
            first = r * TILES_PER_ROUND
            tiles = slice(first, first + TILES_PER_ROUND)
            x_sb = x_pool.tile([P, TILES_PER_ROUND, HID], BF16)
            nc.sync.dma_start(out=x_sb[:], in_=x_view[:, tiles, :])
            tables = x_pool.tile([P, 2, TILES_PER_ROUND, D], BF16)
            nc.sync.dma_start(out=tables[:, COS, :, :], in_=cos_view[:, tiles, :])
            nc.sync.dma_start(out=tables[:, SIN, :, :], in_=sin_view[:, tiles, :])
            x_of[r] = x_sb
            tables_of[r] = tables

        for r in range(LOAD_AHEAD - 3):
            load_tokens(r)

        identity = consts.tile([P, P], F32)
        make_identity(nc, identity[:])
        eps = consts.tile([P, 1], F32)
        nc.vector.memset(eps[:], EPS)
        table_warmer = consts.tile([P, 1], F32)
        nc.scalar.activation(out=table_warmer[:], in_=eps[:], func=ACT.Abs_reciprocal_sqrt)

        def turn(rows_as_words):
            turned = psum_turn.tile([P, TURNS, P], F32)
            for c in range(TURNS):
                nc.tensor.transpose(turned[:, c, :], rows_as_words[:, c * P : (c + 1) * P], identity[:])
            return turned

        def side_by_side(turned):
            return turned[:].rearrange("p (g u) r -> p g r u", u=2)

        w_grouped = consts.tile([P, PASSES, FEATURES, PACK], BF16, align_bytes=64)
        w_grouped_words = w_grouped[:].bitcast(F32)
        w_words = w_raw[:].bitcast(F32)
        for h in range(HEADS):
            turned = turn(w_words[:, h, :])
            copy_out = nc.scalar.copy if h % 2 == 0 else nc.vector.tensor_copy
            copy_out(out=w_grouped_words[:, :, h * D : (h + 1) * D, :], in_=side_by_side(turned))
        w_codes = consts.tile([P, PASSES, FEATURES], U32, align_bytes=64)
        w_scales = consts.tile([P, PASSES, FEATURES], U8, align_bytes=64)
        for g in range(PASSES):
            nc.vector.quantize_mx(
                out=w_codes[:, g, :].bitcast(FP8X4),
                scales=w_scales[:, g, :],
                in_=w_grouped[:, g, :, :].rearrange("p f t -> p (f t)"),
            )

        turned_of = {}
        grouped_of = {}
        codes_of = {}
        product_of = {}
        rstd_of = {}
        result_of = {}
        folded_of = {}
        terms_of = {}
        normed_of = {}

        def transpose_tokens(r):
            x_words = x_of[r][:].bitcast(F32)
            turned_of[r] = [turn(x_words[:, t, :]) for t in range(TILES_PER_ROUND)]

        def regroup(r):
            grouped = stage.tile([P, TILES_PER_ROUND, PASSES, P, PACK], BF16, align_bytes=64)
            grouped_words = grouped[:].bitcast(F32)
            for t in range(TILES_PER_ROUND):
                nc.scalar.copy(out=grouped_words[:, t], in_=side_by_side(turned_of[r][t]))
            grouped_of[r] = grouped

        def quantise(r):
            codes = stats.tile([P, TILES_PER_ROUND, PASSES, P], U32, align_bytes=64)
            scales = stats.tile([P, TILES_PER_ROUND, PASSES, P], U8, align_bytes=64)
            nc.vector.quantize_mx(
                out=codes[:].rearrange("p t g r -> p (t g r)").bitcast(FP8X4),
                scales=scales[:].rearrange("p t g r -> p (t g r)"),
                in_=grouped_of[r][:].rearrange("p t g r v -> p (t g r v)"),
            )
            codes_of[r] = (codes, scales)

        def project(r):
            codes, scales = codes_of[r]
            product_of[r] = []
            for t in range(TILES_PER_ROUND):
                product = psum_prod.tile([P, FEATURES], F32)
                for repeat in range(2):
                    for g in range(PASSES):
                        nc.tensor.matmul_mx(
                            out=product[:],
                            lhsT=codes[:, t, g, :].bitcast(FP8X4),
                            lhsT_scale=scales[:, t, g, :],
                            rhs=w_codes[:, g, :].bitcast(FP8X4),
                            rhs_scale=w_scales[:, g, :],
                            start=(g == 0),
                            stop=(g == PASSES - 1),
                        )
                product_of[r].append(product)

        def norm_factors(r):
            sum_sq = stats.tile([P, HEADS, TILES_PER_ROUND], F32)
            squares = stage.tile([P, HEADS, TILES_PER_ROUND, D], BF16)

            def sum_squares(t, h):
                nc.scalar.activation(
                    out=squares[:, h, t, :],
                    in_=product_of[r][t][:, h * D : (h + 1) * D],
                    func=ACT.Square,
                    accum_out=sum_sq[:, h, t : t + 1],
                )

            def reciprocal_rms(out, sums):
                nc.scalar.activation(out=out, in_=sums, func=ACT.Abs_reciprocal_sqrt, scale=1.0 / D, bias=eps[:])

            sums_in_order = [(t, h) for t in range(TILES_PER_ROUND) for h in (V_HEAD, 0, 1, 2)]
            for t, h in sums_in_order[:-2]:
                sum_squares(t, h)
            rstd_v = stats.tile([P, TILES_PER_ROUND], F32)
            reciprocal_rms(rstd_v[:], sum_sq[:, V_HEAD, :])
            for t, h in sums_in_order[-2:]:
                sum_squares(t, h)
            result = results.tile([P, HEADS, TILES_PER_ROUND, D], F32)
            for t in range(TILES_PER_ROUND):
                nc.scalar.activation(
                    out=result[:, V_HEAD, t, :],
                    in_=product_of[r][t][:, V_HEAD * D : FEATURES],
                    func=ACT.Copy,
                    scale=rstd_v[:, t : t + 1],
                )
            rstd = stats.tile([P, ROTATED, TILES_PER_ROUND], F32)
            reciprocal_rms(rstd[:], sum_sq[:, 0:ROTATED, :])
            rstd_of[r] = rstd
            result_of[r] = result

        low = slice(0, HALF)
        high = slice(HALF, D)
        other_half = ((high, low), (low, high))

        def over_tiles(gain, columns, width):
            return gain[:, columns].unsqueeze(1).to_broadcast([P, TILES_PER_ROUND, width])

        def fold_q_gain(r):
            tables = tables_of[r]
            folded = fold.tile([P, 2, TILES_PER_ROUND, D], F32)
            nc.gpsimd.tensor_tensor(
                out=folded[:, COS, :, :], in0=tables[:, COS, :, :], in1=over_tiles(gain_q, slice(0, D), D), op=ALU.mult
            )
            for here, there in other_half:
                nc.gpsimd.tensor_tensor(
                    out=folded[:, SIN, :, here], in0=tables[:, SIN, :, there], in1=over_tiles(gain_q, here, HALF), op=ALU.mult
                )
            folded_of[r] = folded

        def scale_products(r):
            normed_k = stage.tile([P, TILES_PER_ROUND, D], F32)
            terms = stage.tile([P, 2, ROTATED, TILES_PER_ROUND, D], F32)

            def times_rstd_times(out, t, h, in1):
                nc.vector.scalar_tensor_tensor(
                    out=out,
                    in0=product_of[r][t][:, h * D : (h + 1) * D],
                    scalar=rstd_of[r][:, h, t : t + 1],
                    in1=in1,
                    op0=ALU.mult,
                    op1=ALU.mult,
                )

            for t in range(TILES_PER_ROUND):
                times_rstd_times(normed_k[:, t, :], t, K_HEAD, gain_k[:])
            for t in range(TILES_PER_ROUND):
                for h in range(Q_HEADS):
                    for table in (COS, SIN):
                        times_rstd_times(terms[:, table, h, t, :], t, h, folded_of[r][:, table, t, :])
            normed_of[r] = normed_k
            terms_of[r] = terms

        def rotate_and_store(r):
            first = r * TILES_PER_ROUND
            tiles = slice(first, first + TILES_PER_ROUND)
            tables = tables_of[r]
            normed_k = normed_of[r]
            terms = terms_of[r]
            result = result_of[r]
            nc.vector.tensor_tensor(out=terms[:, COS, K_HEAD, :, :], in0=normed_k[:], in1=tables[:, COS, :, :], op=ALU.mult)
            for here, there in other_half:
                nc.vector.tensor_tensor(
                    out=terms[:, SIN, K_HEAD, :, here], in0=normed_k[:, :, here], in1=tables[:, SIN, :, there], op=ALU.mult
                )
            nc.vector.tensor_tensor(
                out=result[:, 0:ROTATED, :, low], in0=terms[:, COS, :, :, low], in1=terms[:, SIN, :, :, high], op=ALU.subtract
            )
            nc.vector.tensor_tensor(
                out=result[:, 0:ROTATED, :, high], in0=terms[:, COS, :, :, high], in1=terms[:, SIN, :, :, low], op=ALU.add
            )
            nc.sync.dma_start(out=q_view[:, :, tiles, :], in_=result[:, 0:Q_HEADS, :, :])
            nc.sync.dma_start(out=k_view[:, tiles, :], in_=result[:, K_HEAD, :, :])
            nc.sync.dma_start(out=v_view[:, tiles, :], in_=result[:, V_HEAD, :, :])

        def in_range(r):
            return 0 <= r < ROUNDS

        for i in range(-3, ROUNDS):
            if in_range(i + LOAD_AHEAD):
                load_tokens(i + LOAD_AHEAD)
            if in_range(i + 1):
                project(i + 1)
            if in_range(i + 3):
                transpose_tokens(i + 3)
            if in_range(i + 2):
                regroup(i + 2)
            if in_range(i + 1):
                norm_factors(i + 1)
            if in_range(i + 2):
                fold_q_gain(i + 2)
            if in_range(i):
                scale_products(i)
            if in_range(i + 2):
                quantise(i + 2)
            if in_range(i):
                rotate_and_store(i)
